import numpy as np
import ml_dtypes


def mxq(x, axis, fmt="e4m3"):
    dtype, down = {"e4m3": (ml_dtypes.float8_e4m3fn, 7), "e5m2": (ml_dtypes.float8_e5m2, 14)}[fmt]
    v = np.moveaxis(np.asarray(x, np.float32).astype(ml_dtypes.bfloat16).astype(np.float64), axis, -1)
    blocks = v.reshape(v.shape[:-1] + (-1, 32))
    amax = np.abs(blocks).max(-1, keepdims=True)
    byte = np.maximum(np.where(amax > 0, np.frexp(amax)[1] - 1 + 127, 0) - down, 1)
    scale = np.exp2(byte - 127.0)
    codes = (blocks / scale).astype(np.float32).astype(dtype).astype(np.float64)
    return np.moveaxis((codes * scale).reshape(v.shape), -1, axis)


WIDE = False


def mx_kscale(k):
    if not WIDE:
        return np.ones(k)
    levels = np.array([10, -10, 5, -5, 0])
    a = np.random.permutation(np.resize(levels, k // 512 * 4)).reshape(k // 512, 4)
    idx = np.arange(k)
    return np.exp2(a[idx // 512, idx % 128 // 32])


BF16 = ml_dtypes.bfloat16


def bf(x):
    return np.asarray(x, np.float32).astype(BF16)


def f64(x):
    return np.asarray(x).astype(np.float64)


B, C_IN, C_OUT, N, T, K = 2, 512, 128, 512, 12, 3


def cheb_laplacian(p):
    adj = 1.0 / (1.0 + np.exp(-p))
    adj = (adj + adj.T) * 0.5
    adj = adj * (1.0 - np.eye(N))
    deg = adj.sum(axis=1)
    dis = 1.0 / np.sqrt(deg)
    return -(dis[:, None] * adj * dis[None, :])


def setup_inputs():
    s = mx_kscale(C_IN)
    x = np.random.standard_normal((B, C_IN, 1, T)) + np.random.standard_normal((B, C_IN, N, T))
    tx1 = np.random.standard_normal((B, T, 1, C_IN)) + np.random.standard_normal((B, T, N, C_IN)) * 5.0 / np.sqrt(N)
    return {'x': bf(x * s[None, :, None, None]),
            'adj_param': bf(4.0 * np.random.standard_normal((N, N)) - 10.0 + 10.0 * np.eye(N)),
            'tx1': bf(tx1 * s),
            'cheb01': bf(np.random.standard_normal((B, T, N, C_OUT)) * 1.7),
            'w_cheb2': bf(np.random.standard_normal((C_IN, C_OUT)) / np.sqrt(C_IN) / s[:, None]),
            'cheb_bias': bf(np.random.standard_normal(C_OUT) * 0.3)}


def reference(x, adj_param, tx1, cheb01, w_cheb2, cheb_bias):
    s = cheb_laplacian(f64(adj_param))
    xt = f64(x).transpose(0, 3, 2, 1)
    tx2 = 2.0 * (mxq(s, 1, 'e4m3') @ mxq(f64(tx1), 2, 'e4m3')) - xt
    h = f64(cheb01) + (mxq(tx2, 3, 'e4m3') @ mxq(f64(w_cheb2), 0, 'e4m3'))
    h = h + f64(cheb_bias)
    return h.transpose(0, 3, 2, 1)

@@ -1,0 +1,231 @@
+from contextlib import ExitStack
+
+import concourse.mybir as mybir
+from concourse.masks import make_identity
+
+F32 = mybir.dt.float32
+BF16 = mybir.dt.bfloat16
+U32 = mybir.dt.uint32
+U8 = mybir.dt.uint8
+FP8X4 = mybir.dt.float8_e4m3fn_x4
+ALU = mybir.AluOpType
+ACT = mybir.ActivationFunctionType
+
+B, C_IN, C_OUT, N, T = 2, 512, 128, 512, 12
+P = 128
+PACK = 4
+QUAD = 4
+N_QUADS = T // QUAD
+N_BLOCKS = N // P
+assert C_IN == P * PACK and N == P * PACK and C_OUT == P
+
+FLOPS = 2 * B * T * N * N * C_IN + 2 * B * T * N * C_IN * C_OUT
+
+
+def quantise(nc, codes, scales, grouped):
+    nc.vector.quantize_mx(out=codes.bitcast(FP8X4), scales=scales, in_=grouped)
+
+
+def build_constants(tc, nc, banks, ident_bf, adj_param, w_cheb2, cheb_bias, s_codes, s_scales, w_codes, w_scales, bias_col):
+    with tc.tile_pool(name="setup", bufs=1) as setup:
+        adj_rows = setup.tile([P, PACK, N], BF16)
+        nc.sync.dma_start(out=adj_rows[:], in_=adj_param.rearrange("(p j) w -> p j w", j=PACK))
+        w_rows = setup.tile([P, PACK, C_OUT], BF16)
+        nc.sync.dma_start(out=w_rows[:], in_=w_cheb2.rearrange("(k p) o -> p k o", p=P))
+        bias_rows = setup.tile([P, P], BF16)
+        nc.vector.memset(bias_rows[:], 0.0)
+        nc.sync.dma_start(out=bias_rows[0:1, :], in_=cheb_bias.rearrange("(r o) -> r o", r=1))
+
+        ident_f32 = setup.tile([P, P], F32)
+        make_identity(nc, ident_f32[:])
+        diag_sign = setup.tile([P, PACK, N], BF16)
+        nc.gpsimd.memset(diag_sign[:], 1.0)
+        nc.gpsimd.affine_select(
+            out=diag_sign[:],
+            in_=diag_sign[:],
+            compare_op=ALU.not_equal,
+            fill=-1.0,
+            base=0,
+            pattern=[[1, PACK], [-1, N]],
+            channel_multiplier=PACK,
+        )
+
+        sig = setup.tile([P, PACK, N], F32)
+        nc.scalar.activation(out=sig[:], in_=adj_rows[:], func=ACT.Sigmoid)
+
+        adj_words = adj_rows[:].bitcast(F32).rearrange("q jj (p u) -> q jj p u", u=2)
+        sig_t = setup.tile([P, PACK, N], F32)
+        for u in range(2):
+            adj_t = banks.tile([P, PACK, P], F32, tag="turn")
+            for jj in range(PACK):
+                nc.tensor.transpose(adj_t[:, jj, :], adj_words[:, jj, :, u], ident_f32[:])
+            nc.scalar.activation(
+                out=sig_t[:, 2 * u : 2 * u + 2, :].rearrange("p e (q jj) -> p e q jj", jj=PACK),
+                in_=adj_t[:].bitcast(BF16).rearrange("p jj (q e) -> p e q jj", e=2),
+                func=ACT.Sigmoid,
+            )
+
+        nc.vector.tensor_tensor(out=sig[:], in0=sig[:], in1=diag_sign[:], op=ALU.mult)
+        both = sig
+        row_sum = setup.tile([P, PACK], F32)
+        for j in range(PACK):
+            nc.vector.scalar_tensor_tensor(
+                out=both[:, j, :],
+                in0=sig[:, j, :],
+                scalar=1.0,
+                in1=sig_t[:, j, :],
+                op0=ALU.mult,
+                op1=ALU.add,
+                accum_out=row_sum[:, j : j + 1],
+            )
+
+        root = setup.tile([P, PACK], F32)
+        nc.scalar.activation(out=root[:], in_=row_sum[:], func=ACT.Sqrt, scale=0.5)
+        dis = setup.tile([P, PACK], F32)
+        nc.vector.reciprocal(out=dis[:], in_=root[:])
+        neg_half_dis = setup.tile([P, PACK], F32)
+        nc.vector.tensor_scalar_mul(out=neg_half_dis[:], in0=dis[:], scalar1=-0.5)
+        dis_cols = banks.tile([P, PACK, P], F32, tag="small")
+        for jj in range(PACK):
+            nc.tensor.matmul(
+                out=dis_cols[:, jj, :],
+                lhsT=dis[:, jj : jj + 1].to_broadcast([P, P]),
+                rhs=ident_f32[:],
+                start=True,
+                stop=True,
+            )
+        s_rows = both
+        for j in range(PACK):
+            nc.vector.scalar_tensor_tensor(
+                out=s_rows[:, j, :].rearrange("p (q jj) -> p q jj", jj=PACK),
+                in0=both[:, j, :].rearrange("p (q jj) -> p q jj", jj=PACK),
+                scalar=neg_half_dis[:, j : j + 1],
+                in1=dis_cols[:].rearrange("p jj q -> p q jj"),
+                op0=ALU.mult,
+                op1=ALU.mult,
+            )
+        s_grouped = setup.tile([P, N, PACK], BF16, align_bytes=64)
+        for vb in range(N_BLOCKS):
+            v_cols = slice(vb * P, (vb + 1) * P)
+            nc.vector.tensor_copy(out=s_grouped[:, v_cols, :], in_=s_rows[:, :, v_cols].rearrange("p j v -> p v j"))
+            quantise(nc, s_codes[:, v_cols], s_scales[:, v_cols], s_grouped[:, v_cols, :].rearrange("p v j -> p (v j)"))
+
+        w_grouped = setup.tile([P, C_OUT, PACK], BF16, align_bytes=64)
+        nc.vector.tensor_copy(out=w_grouped[:], in_=w_rows[:].rearrange("p k o -> p o k"))
+        quantise(nc, w_codes[:], w_scales[:], w_grouped[:].rearrange("p o k -> p (o k)"))
+
+        bias_t = banks.tile([P, P], BF16, tag="small")
+        nc.tensor.transpose(bias_t[:], bias_rows[:], ident_bf[:])
+        nc.vector.tensor_copy(out=bias_col[:], in_=bias_t[:, 0:1])
+
+
+def tile_dynamicgraphspatialconv_pb_t_kernel(tc, x, adj_param, tx1, cheb01, w_cheb2, cheb_bias, out):
+    nc = tc.nc
+    with ExitStack() as pools:
+        keep = pools.enter_context(tc.tile_pool(name="keep", bufs=1))
+        banks = pools.enter_context(tc.psum_pool(name="banks", bufs=2))
+        tx1_pool = pools.enter_context(tc.tile_pool(name="tx1", bufs=2))
+        x_pool = pools.enter_context(tc.tile_pool(name="x", bufs=3))
+        unit_pool = pools.enter_context(tc.tile_pool(name="unit", bufs=2))
+
+        ident_bf = keep.tile([P, P], BF16)
+        make_identity(nc, ident_bf[:])
+        s_codes = keep.tile([P, N], U32, align_bytes=64)
+        s_scales = keep.tile([P, N], U8, align_bytes=64)
+        w_codes = keep.tile([P, C_OUT], U32, align_bytes=64)
+        w_scales = keep.tile([P, C_OUT], U8, align_bytes=64)
+        bias_col = keep.tile([P, 1], F32)
+        build_constants(tc, nc, banks, ident_bf, adj_param, w_cheb2, cheb_bias, s_codes, s_scales, w_codes, w_scales, bias_col)
+
+        out_pool = pools.enter_context(tc.tile_pool(name="out", bufs=N_BLOCKS + 2))
+
+        for b in range(B):
+            x_rows = x[b].rearrange("(k p) v t -> p k (v t)", p=P)
+            x_blocks = []
+            out_blocks = []
+            for quad in range(N_QUADS):
+                steps = slice(quad * QUAD, (quad + 1) * QUAD)
+
+                tx1_codes = tx1_pool.tile([P, QUAD, C_IN], U32, align_bytes=64)
+                tx1_scales = tx1_pool.tile([P, QUAD, C_IN], U8, align_bytes=64)
+                for i in range(QUAD):
+                    tx1_rows = tx1_pool.tile([P, PACK, C_IN], BF16, bufs=4)
+                    nc.sync.dma_start(out=tx1_rows[:], in_=tx1[b, quad * QUAD + i].rearrange("(p j) c -> p j c", j=PACK))
+                    tx1_grouped = tx1_pool.tile([P, C_IN, PACK], BF16, bufs=3, align_bytes=64)
+                    nc.scalar.copy(
+                        out=tx1_grouped[:].rearrange("p (c r) j -> p c j r", r=4),
+                        in_=tx1_rows[:].rearrange("p j (c r) -> p c j r", r=4),
+                    )
+                    quantise(nc, tx1_codes[:, i, :], tx1_scales[:, i, :], tx1_grouped[:].rearrange("p c j -> p (c j)"))
+
+                for vb in range(N_BLOCKS):
+                    v_cols = slice(vb * P, (vb + 1) * P)
+                    if quad == 0:
+                        x_block = x_pool.tile([P, PACK, P * T], BF16, bufs=N_BLOCKS + 2)
+                        nc.sync.dma_start(out=x_block[:], in_=x_rows[:, :, vb * P * T : (vb + 1) * P * T])
+                        x_blocks.append(x_block)
+                        out_block = out_pool.tile([P, P, T], F32)
+                        out_blocks.append(out_block)
+
+                    cheb_rows = unit_pool.tile([P, QUAD, C_OUT], BF16)
+                    nc.sync.dma_start(out=cheb_rows[:], in_=cheb01[b, steps, v_cols, :].rearrange("t v o -> v t o"))
+                    cheb_bank = banks.tile([P, QUAD, P], BF16, tag="turn")
+                    for i in range(QUAD):
+                        nc.tensor.transpose(cheb_bank[:, i, :], cheb_rows[:, i, :], ident_bf[:])
+                    cheb_t = unit_pool.tile([P, QUAD, P], BF16)
+                    nc.scalar.copy(out=cheb_t[:], in_=cheb_bank[:])
+
+                    x_quad = x_pool.tile([P, P, PACK, QUAD], BF16)
+                    nc.scalar.copy(
+                        out=x_quad[:].bitcast(F32),
+                        in_=x_blocks[vb][:]
+                        .bitcast(F32)
+                        .rearrange("p k (v w) -> p v k w", w=T // 2)[:, :, :, quad * 2 : quad * 2 + 2],
+                    )
+
+                    tx2_grouped = unit_pool.tile([P, QUAD, P, PACK], BF16, align_bytes=64)
+                    for i in range(QUAD):
+                        product = banks.tile([P, PACK, P], F32, tag="first", bufs=4)
+                        for k in range(PACK):
+                            c_cols = slice(k * P, (k + 1) * P)
+                            nc.tensor.matmul_mx(
+                                out=product[:, k, :],
+                                lhsT=tx1_codes[:, i, c_cols].bitcast(FP8X4),
+                                lhsT_scale=tx1_scales[:, i, c_cols],
+                                rhs=s_codes[:, v_cols].bitcast(FP8X4),
+                                rhs_scale=s_scales[:, v_cols],
+                                start=True,
+                                stop=True,
+                            )
+                        nc.vector.scalar_tensor_tensor(
+                            out=tx2_grouped[:, i, :, :],
+                            in0=product[:].rearrange("p k v -> p v k"),
+                            scalar=2.0,
+                            in1=x_quad[:, :, :, i],
+                            op0=ALU.mult,
+                            op1=ALU.subtract,
+                        )
+                    tx2_codes = unit_pool.tile([P, QUAD * P], U32, align_bytes=64)
+                    tx2_scales = unit_pool.tile([P, QUAD * P], U8, align_bytes=64)
+                    quantise(nc, tx2_codes[:], tx2_scales[:], tx2_grouped[:].rearrange("p i v k -> p (i v k)"))
+
+                    mixed = banks.tile([P, QUAD, P], F32, tag="small")
+                    nc.tensor.matmul_mx(
+                        out=mixed[:].rearrange("o i v -> o (i v)"),
+                        lhsT=w_codes[:].bitcast(FP8X4),
+                        lhsT_scale=w_scales[:],
+                        rhs=tx2_codes[:].bitcast(FP8X4),
+                        rhs_scale=tx2_scales[:],
+                        start=True,
+                        stop=True,
+                    )
+                    nc.vector.scalar_tensor_tensor(
+                        out=out_blocks[vb][:, :, steps],
+                        in0=mixed[:].rearrange("o i v -> o v i"),
+                        scalar=bias_col[:, 0:1],
+                        in1=cheb_t[:].rearrange("o i v -> o v i"),
+                        op0=ALU.add,
+                        op1=ALU.add,
+                    )
+                    if quad == N_QUADS - 1:
+                        nc.sync.dma_start(out=out[b, :, v_cols, :], in_=out_blocks[vb][:])

@@ -19,6 +19,18 @@ N_QUADS = T // QUAD
 N_BLOCKS = N // P
 assert C_IN == P * PACK and N == P * PACK and C_OUT == P
 
+UNITS = [(b, quad, vb) for b in range(B) for quad in range(N_QUADS) for vb in range(N_BLOCKS)]
+N_UNITS = len(UNITS)
+N_STEPS = B * T
+assert N_BLOCKS == QUAD and N_UNITS == N_STEPS
+
+STEP_LOAD_AHEAD = 10
+STEP_REGROUP_AHEAD = 6
+STEP_QUANTISE_AHEAD = 5
+UNIT_LOAD_AHEAD = 6
+UNIT_MOVE_AHEAD = 2
+VECTOR_REGROUPS = QUAD
+
 FLOPS = 2 * B * T * N * N * C_IN + 2 * B * T * N * C_IN * C_OUT
 
 
@@ -50,64 +62,59 @@ def build_constants(tc, nc, banks, ident_bf, adj_param, w_cheb2, cheb_bias, s_co
             channel_multiplier=PACK,
         )
 
-        sig = setup.tile([P, PACK, N], F32)
-        nc.scalar.activation(out=sig[:], in_=adj_rows[:], func=ACT.Sigmoid)
-
-        adj_words = adj_rows[:].bitcast(F32).rearrange("q jj (p u) -> q jj p u", u=2)
-        sig_t = setup.tile([P, PACK, N], F32)
-        for u in range(2):
-            adj_t = banks.tile([P, PACK, P], F32, tag="turn")
+        adj_words = adj_rows[:].bitcast(F32).rearrange("q jj (p h) -> q jj p h", h=2)
+        adj_t = []
+        for h in range(2):
+            adj_t_half = banks.tile([P, PACK, P], F32, tag="turn")
             for jj in range(PACK):
-                nc.tensor.transpose(adj_t[:, jj, :], adj_words[:, jj, :, u], ident_f32[:])
+                nc.tensor.transpose(adj_t_half[:, jj, :], adj_words[:, jj, :, h], ident_f32[:])
+            adj_t.append(adj_t_half)
+
+        graph = setup.tile([P, PACK, N], F32)
+        sig_t = setup.tile([P, PACK, N], F32)
+        row_sum = setup.tile([P, PACK], F32)
+        for h in range(2):
+            rows = slice(2 * h, 2 * h + 2)
+            nc.scalar.activation(out=graph[:, rows, :], in_=adj_rows[:, rows, :], func=ACT.Sigmoid)
             nc.scalar.activation(
-                out=sig_t[:, 2 * u : 2 * u + 2, :].rearrange("p e (q jj) -> p e q jj", jj=PACK),
-                in_=adj_t[:].bitcast(BF16).rearrange("p jj (q e) -> p e q jj", e=2),
+                out=sig_t[:, rows, :].rearrange("p e (q jj) -> p e q jj", jj=PACK),
+                in_=adj_t[h][:].bitcast(BF16).rearrange("p jj (q e) -> p e q jj", e=2),
                 func=ACT.Sigmoid,
             )
-
-        nc.vector.tensor_tensor(out=sig[:], in0=sig[:], in1=diag_sign[:], op=ALU.mult)
-        both = sig
-        row_sum = setup.tile([P, PACK], F32)
-        for j in range(PACK):
-            nc.vector.scalar_tensor_tensor(
-                out=both[:, j, :],
-                in0=sig[:, j, :],
-                scalar=1.0,
-                in1=sig_t[:, j, :],
-                op0=ALU.mult,
-                op1=ALU.add,
-                accum_out=row_sum[:, j : j + 1],
-            )
-
+            nc.vector.tensor_tensor(out=graph[:, rows, :], in0=graph[:, rows, :], in1=diag_sign[:, rows, :], op=ALU.mult)
+            for j in range(2 * h, 2 * h + 2):
+                nc.vector.scalar_tensor_tensor(
+                    out=graph[:, j, :],
+                    in0=graph[:, j, :],
+                    scalar=1.0,
+                    in1=sig_t[:, j, :],
+                    op0=ALU.mult,
+                    op1=ALU.add,
+                    accum_out=row_sum[:, j : j + 1],
+                )
         root = setup.tile([P, PACK], F32)
+        nc.scalar.activation(out=root[:, 0:1], in_=sig_t[:, PACK - 1, 0:1], func=ACT.Sqrt)
+
         nc.scalar.activation(out=root[:], in_=row_sum[:], func=ACT.Sqrt, scale=0.5)
         dis = setup.tile([P, PACK], F32)
         nc.vector.reciprocal(out=dis[:], in_=root[:])
-        neg_half_dis = setup.tile([P, PACK], F32)
-        nc.vector.tensor_scalar_mul(out=neg_half_dis[:], in0=dis[:], scalar1=-0.5)
-        dis_cols = banks.tile([P, PACK, P], F32, tag="small")
+        repeated = setup.tile([P, PACK, P], F32)
+        nc.vector.tensor_scalar_mul(out=repeated[:], in0=dis[:].unsqueeze(2).to_broadcast([P, PACK, P]), scalar1=-0.5)
+        col_factor = banks.tile([P, PACK, P], F32, tag="small")
         for jj in range(PACK):
-            nc.tensor.matmul(
-                out=dis_cols[:, jj, :],
-                lhsT=dis[:, jj : jj + 1].to_broadcast([P, P]),
-                rhs=ident_f32[:],
-                start=True,
-                stop=True,
-            )
-        s_rows = both
+            nc.tensor.transpose(col_factor[:, jj, :], repeated[:, jj, :], ident_f32[:])
         for j in range(PACK):
-            nc.vector.scalar_tensor_tensor(
-                out=s_rows[:, j, :].rearrange("p (q jj) -> p q jj", jj=PACK),
-                in0=both[:, j, :].rearrange("p (q jj) -> p q jj", jj=PACK),
-                scalar=neg_half_dis[:, j : j + 1],
-                in1=dis_cols[:].rearrange("p jj q -> p q jj"),
-                op0=ALU.mult,
-                op1=ALU.mult,
-            )
+            nc.vector.tensor_scalar_mul(out=graph[:, j, :], in0=graph[:, j, :], scalar1=dis[:, j : j + 1])
         s_grouped = setup.tile([P, N, PACK], BF16, align_bytes=64)
         for vb in range(N_BLOCKS):
             v_cols = slice(vb * P, (vb + 1) * P)
-            nc.vector.tensor_copy(out=s_grouped[:, v_cols, :], in_=s_rows[:, :, v_cols].rearrange("p j v -> p v j"))
+            q_cols = slice(vb * P // PACK, (vb + 1) * P // PACK)
+            nc.vector.tensor_tensor(
+                out=s_grouped[:, v_cols, :].rearrange("p (q jj) j -> p q jj j", jj=PACK),
+                in0=graph[:, :, v_cols].rearrange("p j (q jj) -> p q jj j", jj=PACK),
+                in1=col_factor[:, :, q_cols].rearrange("p jj q -> p q jj").unsqueeze(3).to_broadcast([P, P // PACK, PACK, PACK]),
+                op=ALU.mult,
+            )
             quantise(nc, s_codes[:, v_cols], s_scales[:, v_cols], s_grouped[:, v_cols, :].rearrange("p v j -> p (v j)"))
 
         w_grouped = setup.tile([P, C_OUT, PACK], BF16, align_bytes=64)
@@ -124,9 +131,7 @@ def tile_dynamicgraphspatialconv_pb_t_kernel(tc, x, adj_param, tx1, cheb01, w_ch
     with ExitStack() as pools:
         keep = pools.enter_context(tc.tile_pool(name="keep", bufs=1))
         banks = pools.enter_context(tc.psum_pool(name="banks", bufs=2))
-        tx1_pool = pools.enter_context(tc.tile_pool(name="tx1", bufs=2))
-        x_pool = pools.enter_context(tc.tile_pool(name="x", bufs=3))
-        unit_pool = pools.enter_context(tc.tile_pool(name="unit", bufs=2))
+        work = pools.enter_context(tc.tile_pool(name="work", bufs=2))
 
         ident_bf = keep.tile([P, P], BF16)
         make_identity(nc, ident_bf[:])
@@ -139,93 +144,152 @@ def tile_dynamicgraphspatialconv_pb_t_kernel(tc, x, adj_param, tx1, cheb01, w_ch
 
         out_pool = pools.enter_context(tc.tile_pool(name="out", bufs=N_BLOCKS + 2))
 
-        for b in range(B):
-            x_rows = x[b].rearrange("(k p) v t -> p k (v t)", p=P)
-            x_blocks = []
-            out_blocks = []
-            for quad in range(N_QUADS):
-                steps = slice(quad * QUAD, (quad + 1) * QUAD)
+        step_rows, step_grouped, quad_codes, quad_scales = {}, {}, {}, {}
+        unit_cheb_rows, unit_cheb_t, unit_x_quad, unit_products, unit_grouped, unit_mixed = {}, {}, {}, {}, {}, {}
+        x_blocks, out_blocks = {}, {}
 
-                tx1_codes = tx1_pool.tile([P, QUAD, C_IN], U32, align_bytes=64)
-                tx1_scales = tx1_pool.tile([P, QUAD, C_IN], U8, align_bytes=64)
-                for i in range(QUAD):
-                    tx1_rows = tx1_pool.tile([P, PACK, C_IN], BF16, bufs=4)
-                    nc.sync.dma_start(out=tx1_rows[:], in_=tx1[b, quad * QUAD + i].rearrange("(p j) c -> p j c", j=PACK))
-                    tx1_grouped = tx1_pool.tile([P, C_IN, PACK], BF16, bufs=3, align_bytes=64)
-                    nc.scalar.copy(
-                        out=tx1_grouped[:].rearrange("p (c r) j -> p c j r", r=4),
-                        in_=tx1_rows[:].rearrange("p j (c r) -> p c j r", r=4),
-                    )
-                    quantise(nc, tx1_codes[:, i, :], tx1_scales[:, i, :], tx1_grouped[:].rearrange("p c j -> p (c j)"))
+        def load_step(s):
+            tx1_rows = work.tile([P, PACK, C_IN], BF16, bufs=STEP_LOAD_AHEAD - STEP_REGROUP_AHEAD + 2)
+            nc.sync.dma_start(out=tx1_rows[:], in_=tx1[s // T, s % T].rearrange("(p j) c -> p j c", j=PACK))
+            step_rows[s] = tx1_rows
 
-                for vb in range(N_BLOCKS):
-                    v_cols = slice(vb * P, (vb + 1) * P)
-                    if quad == 0:
-                        x_block = x_pool.tile([P, PACK, P * T], BF16, bufs=N_BLOCKS + 2)
-                        nc.sync.dma_start(out=x_block[:], in_=x_rows[:, :, vb * P * T : (vb + 1) * P * T])
-                        x_blocks.append(x_block)
-                        out_block = out_pool.tile([P, P, T], F32)
-                        out_blocks.append(out_block)
+        def regroup_step(s):
+            tx1_grouped = work.tile([P, C_IN, PACK], BF16, bufs=STEP_REGROUP_AHEAD - STEP_QUANTISE_AHEAD + 2, align_bytes=64)
+            grouped_view = tx1_grouped[:].rearrange("p (c r) j -> p c j r", r=4)
+            rows_view = step_rows[s][:].rearrange("p j (c r) -> p c j r", r=4)
+            if s < VECTOR_REGROUPS:
+                nc.vector.tensor_copy(out=grouped_view, in_=rows_view)
+            else:
+                nc.scalar.copy(out=grouped_view, in_=rows_view)
+            step_grouped[s] = tx1_grouped
 
-                    cheb_rows = unit_pool.tile([P, QUAD, C_OUT], BF16)
-                    nc.sync.dma_start(out=cheb_rows[:], in_=cheb01[b, steps, v_cols, :].rearrange("t v o -> v t o"))
-                    cheb_bank = banks.tile([P, QUAD, P], BF16, tag="turn")
-                    for i in range(QUAD):
-                        nc.tensor.transpose(cheb_bank[:, i, :], cheb_rows[:, i, :], ident_bf[:])
-                    cheb_t = unit_pool.tile([P, QUAD, P], BF16)
-                    nc.scalar.copy(out=cheb_t[:], in_=cheb_bank[:])
+        def quantise_step(s):
+            g, i = s // QUAD, s % QUAD
+            if i == 0:
+                tx1_codes = work.tile([P, QUAD, C_IN], U32, align_bytes=64)
+                tx1_scales = work.tile([P, QUAD, C_IN], U8, align_bytes=64)
+                quad_codes[g], quad_scales[g] = tx1_codes, tx1_scales
+            quantise(nc, quad_codes[g][:, i, :], quad_scales[g][:, i, :], step_grouped[s][:].rearrange("p c j -> p (c j)"))
 
-                    x_quad = x_pool.tile([P, P, PACK, QUAD], BF16)
-                    nc.scalar.copy(
-                        out=x_quad[:].bitcast(F32),
-                        in_=x_blocks[vb][:]
-                        .bitcast(F32)
-                        .rearrange("p k (v w) -> p v k w", w=T // 2)[:, :, :, quad * 2 : quad * 2 + 2],
-                    )
+        def load_unit(u):
+            b, quad, vb = UNITS[u]
+            if quad == 0:
+                x_block = work.tile([P, PACK, P * T], BF16, bufs=N_BLOCKS + 2)
+                nc.sync.dma_start(
+                    out=x_block[:],
+                    in_=x[b].rearrange("(k p) v t -> p k (v t)", p=P)[:, :, vb * P * T : (vb + 1) * P * T],
+                )
+                x_blocks[(b, vb)] = x_block
+            cheb_rows = work.tile([P, QUAD, C_OUT], BF16, bufs=UNIT_LOAD_AHEAD - UNIT_MOVE_AHEAD + 2)
+            nc.sync.dma_start(
+                out=cheb_rows[:],
+                in_=cheb01[b, quad * QUAD : (quad + 1) * QUAD, vb * P : (vb + 1) * P, :].rearrange("t v o -> v t o"),
+            )
+            unit_cheb_rows[u] = cheb_rows
 
-                    tx2_grouped = unit_pool.tile([P, QUAD, P, PACK], BF16, align_bytes=64)
-                    for i in range(QUAD):
-                        product = banks.tile([P, PACK, P], F32, tag="first", bufs=4)
-                        for k in range(PACK):
-                            c_cols = slice(k * P, (k + 1) * P)
-                            nc.tensor.matmul_mx(
-                                out=product[:, k, :],
-                                lhsT=tx1_codes[:, i, c_cols].bitcast(FP8X4),
-                                lhsT_scale=tx1_scales[:, i, c_cols],
-                                rhs=s_codes[:, v_cols].bitcast(FP8X4),
-                                rhs_scale=s_scales[:, v_cols],
-                                start=True,
-                                stop=True,
-                            )
-                        nc.vector.scalar_tensor_tensor(
-                            out=tx2_grouped[:, i, :, :],
-                            in0=product[:].rearrange("p k v -> p v k"),
-                            scalar=2.0,
-                            in1=x_quad[:, :, :, i],
-                            op0=ALU.mult,
-                            op1=ALU.subtract,
-                        )
-                    tx2_codes = unit_pool.tile([P, QUAD * P], U32, align_bytes=64)
-                    tx2_scales = unit_pool.tile([P, QUAD * P], U8, align_bytes=64)
-                    quantise(nc, tx2_codes[:], tx2_scales[:], tx2_grouped[:].rearrange("p i v k -> p (i v k)"))
+        def move_unit(u):
+            b, quad, vb = UNITS[u]
+            cheb_bank = banks.tile([P, QUAD, P], BF16, tag="turn")
+            for i in range(QUAD):
+                nc.tensor.transpose(cheb_bank[:, i, :], unit_cheb_rows[u][:, i, :], ident_bf[:])
+            cheb_t = work.tile([P, QUAD, P], BF16, bufs=UNIT_MOVE_AHEAD + 3)
+            nc.scalar.copy(out=cheb_t[:], in_=cheb_bank[:])
+            unit_cheb_t[u] = cheb_t
+            x_quad = work.tile([P, P, PACK, QUAD], BF16, bufs=UNIT_MOVE_AHEAD + 2)
+            nc.scalar.copy(
+                out=x_quad[:].bitcast(F32),
+                in_=x_blocks[(b, vb)][:]
+                .bitcast(F32)
+                .rearrange("p k (v w) -> p v k w", w=T // 2)[:, :, :, quad * 2 : quad * 2 + 2],
+            )
+            unit_x_quad[u] = x_quad
 
-                    mixed = banks.tile([P, QUAD, P], F32, tag="small")
-                    nc.tensor.matmul_mx(
-                        out=mixed[:].rearrange("o i v -> o (i v)"),
-                        lhsT=w_codes[:].bitcast(FP8X4),
-                        lhsT_scale=w_scales[:],
-                        rhs=tx2_codes[:].bitcast(FP8X4),
-                        rhs_scale=tx2_scales[:],
-                        start=True,
-                        stop=True,
-                    )
-                    nc.vector.scalar_tensor_tensor(
-                        out=out_blocks[vb][:, :, steps],
-                        in0=mixed[:].rearrange("o i v -> o v i"),
-                        scalar=bias_col[:, 0:1],
-                        in1=cheb_t[:].rearrange("o i v -> o v i"),
-                        op0=ALU.add,
-                        op1=ALU.add,
-                    )
-                    if quad == N_QUADS - 1:
-                        nc.sync.dma_start(out=out[b, :, v_cols, :], in_=out_blocks[vb][:])
+        def first_matmul(u, i):
+            vb = UNITS[u][2]
+            v_cols = slice(vb * P, (vb + 1) * P)
+            g = u // N_BLOCKS
+            product = banks.tile([P, PACK, P], F32, tag="first", bufs=QUAD)
+            for k in range(PACK):
+                c_cols = slice(k * P, (k + 1) * P)
+                nc.tensor.matmul_mx(
+                    out=product[:, k, :],
+                    lhsT=quad_codes[g][:, i, c_cols].bitcast(FP8X4),
+                    lhsT_scale=quad_scales[g][:, i, c_cols],
+                    rhs=s_codes[:, v_cols].bitcast(FP8X4),
+                    rhs_scale=s_scales[:, v_cols],
+                    start=True,
+                    stop=True,
+                )
+            unit_products[(u, i)] = product
+
+        def subtract_x(u, i):
+            if i == 0:
+                tx2_grouped = work.tile([P, QUAD, P, PACK], BF16, align_bytes=64)
+                unit_grouped[u] = tx2_grouped
+            nc.vector.scalar_tensor_tensor(
+                out=unit_grouped[u][:, i, :, :],
+                in0=unit_products[(u, i)][:].rearrange("p k v -> p v k"),
+                scalar=2.0,
+                in1=unit_x_quad[u][:, :, :, i],
+                op0=ALU.mult,
+                op1=ALU.subtract,
+            )
+
+        def second_matmul(u):
+            tx2_codes = work.tile([P, QUAD * P], U32, align_bytes=64)
+            tx2_scales = work.tile([P, QUAD * P], U8, align_bytes=64)
+            quantise(nc, tx2_codes[:], tx2_scales[:], unit_grouped[u][:].rearrange("p i v k -> p (i v k)"))
+            mixed = banks.tile([P, QUAD, P], F32, tag="small")
+            nc.tensor.matmul_mx(
+                out=mixed[:].rearrange("o i v -> o (i v)"),
+                lhsT=w_codes[:].bitcast(FP8X4),
+                lhsT_scale=w_scales[:],
+                rhs=tx2_codes[:].bitcast(FP8X4),
+                rhs_scale=tx2_scales[:],
+                start=True,
+                stop=True,
+            )
+            unit_mixed[u] = mixed
+
+        def finish_unit(u):
+            b, quad, vb = UNITS[u]
+            if quad == 0:
+                out_block = out_pool.tile([P, P, T], F32)
+                out_blocks[(b, vb)] = out_block
+            nc.vector.scalar_tensor_tensor(
+                out=out_blocks[(b, vb)][:, :, quad * QUAD : (quad + 1) * QUAD],
+                in0=unit_mixed[u][:].rearrange("o i v -> o v i"),
+                scalar=bias_col[:, 0:1],
+                in1=unit_cheb_t[u][:].rearrange("o i v -> o v i"),
+                op0=ALU.add,
+                op1=ALU.add,
+            )
+            if quad == N_QUADS - 1:
+                nc.sync.dma_start(out=out[b, :, vb * P : (vb + 1) * P, :], in_=out_blocks[(b, vb)][:])
+
+        def run_round(u):
+            if 0 <= u + STEP_LOAD_AHEAD < N_STEPS:
+                load_step(u + STEP_LOAD_AHEAD)
+            if 0 <= u + UNIT_LOAD_AHEAD < N_UNITS:
+                load_unit(u + UNIT_LOAD_AHEAD)
+            if 0 <= u + STEP_REGROUP_AHEAD < N_STEPS:
+                regroup_step(u + STEP_REGROUP_AHEAD)
+            if 0 <= u + UNIT_MOVE_AHEAD < N_UNITS:
+                move_unit(u + UNIT_MOVE_AHEAD)
+            for i in range(QUAD):
+                if 0 <= u < N_UNITS:
+                    subtract_x(u, i)
+                if 0 <= u + 1 < N_UNITS:
+                    first_matmul(u + 1, i)
+            if 0 <= u + STEP_QUANTISE_AHEAD < N_STEPS:
+                quantise_step(u + STEP_QUANTISE_AHEAD)
+            if 0 <= u < N_UNITS:
+                second_matmul(u)
+            if 0 <= u - 1 < N_UNITS:
+                finish_unit(u - 1)
+
+        for u in range(-STEP_LOAD_AHEAD, 0):
+            run_round(u)
+        with tc.manual_schedule():
+            for u in range(0, N_UNITS + 1):
+                run_round(u)

@@ -50,50 +50,44 @@ def build_constants(tc, nc, banks, ident_bf, adj_param, w_cheb2, cheb_bias, s_co
 
         ident_f32 = setup.tile([P, P], F32)
         make_identity(nc, ident_f32[:])
-        diag_sign = setup.tile([P, PACK, N], BF16)
-        nc.gpsimd.memset(diag_sign[:], 1.0)
-        nc.gpsimd.affine_select(
-            out=diag_sign[:],
-            in_=diag_sign[:],
-            compare_op=ALU.not_equal,
-            fill=-1.0,
-            base=0,
-            pattern=[[1, PACK], [-1, N]],
-            channel_multiplier=PACK,
-        )
+        make_identity(nc, ident_bf[:])
 
-        adj_words = adj_rows[:].bitcast(F32).rearrange("q jj (p h) -> q jj p h", h=2)
-        adj_t = []
-        for h in range(2):
-            adj_t_half = banks.tile([P, PACK, P], F32, tag="turn")
-            for jj in range(PACK):
-                nc.tensor.transpose(adj_t_half[:, jj, :], adj_words[:, jj, :, h], ident_f32[:])
-            adj_t.append(adj_t_half)
-
-        graph = setup.tile([P, PACK, N], F32)
-        sig_t = setup.tile([P, PACK, N], F32)
-        row_sum = setup.tile([P, PACK], F32)
-        for h in range(2):
-            rows = slice(2 * h, 2 * h + 2)
-            nc.scalar.activation(out=graph[:, rows, :], in_=adj_rows[:, rows, :], func=ACT.Sigmoid)
+        sig = setup.tile([P, PACK, PACK, P], F32)
+        sig_t = []
+        for cls in range(PACK):
             nc.scalar.activation(
-                out=sig_t[:, rows, :].rearrange("p e (q jj) -> p e q jj", jj=PACK),
-                in_=adj_t[h][:].bitcast(BF16).rearrange("p jj (q e) -> p e q jj", e=2),
+                out=sig[:, cls, :, :],
+                in_=adj_rows[:].rearrange("q jj (m cls) -> q cls jj m", cls=PACK)[:, cls, :, :],
                 func=ACT.Sigmoid,
             )
-            nc.vector.tensor_tensor(out=graph[:, rows, :], in0=graph[:, rows, :], in1=diag_sign[:, rows, :], op=ALU.mult)
-            for j in range(2 * h, 2 * h + 2):
-                nc.vector.scalar_tensor_tensor(
-                    out=graph[:, j, :],
-                    in0=graph[:, j, :],
-                    scalar=1.0,
-                    in1=sig_t[:, j, :],
-                    op0=ALU.mult,
-                    op1=ALU.add,
-                    accum_out=row_sum[:, j : j + 1],
-                )
+            nc.gpsimd.affine_select(
+                out=sig[:, cls, :, :],
+                in_=sig[:, cls, :, :],
+                compare_op=ALU.not_equal,
+                fill=0.0,
+                base=-cls,
+                pattern=[[1, PACK], [-PACK, P]],
+                channel_multiplier=PACK,
+            )
+            sig_t_rows = banks.tile([P, PACK, P], F32, tag="first", bufs=QUAD)
+            for jj in range(PACK):
+                nc.tensor.transpose(sig_t_rows[:, jj, :], sig[:, cls, jj, :], ident_f32[:])
+            sig_t.append(sig_t_rows)
+
+        graph = setup.tile([P, PACK, N], F32)
+        row_sum = setup.tile([P, PACK], F32)
+        for j in range(PACK):
+            nc.vector.scalar_tensor_tensor(
+                out=graph[:, j, :].rearrange("p (m cls) -> p m cls", cls=PACK),
+                in0=sig[:, :, j, :].rearrange("p cls m -> p m cls"),
+                scalar=1.0,
+                in1=sig_t[j][:].rearrange("p cls m -> p m cls"),
+                op0=ALU.mult,
+                op1=ALU.add,
+                accum_out=row_sum[:, j : j + 1],
+            )
         root = setup.tile([P, PACK], F32)
-        nc.scalar.activation(out=root[:, 0:1], in_=sig_t[:, PACK - 1, 0:1], func=ACT.Sqrt)
+        nc.scalar.activation(out=root[:, 0:1], in_=sig[:, PACK - 1, 0, 0:1], func=ACT.Sqrt)
 
         nc.scalar.activation(out=root[:], in_=row_sum[:], func=ACT.Sqrt, scale=0.5)
         dis = setup.tile([P, PACK], F32)
@@ -104,7 +98,7 @@ def build_constants(tc, nc, banks, ident_bf, adj_param, w_cheb2, cheb_bias, s_co
         for jj in range(PACK):
             nc.tensor.transpose(col_factor[:, jj, :], repeated[:, jj, :], ident_f32[:])
         for j in range(PACK):
-            nc.vector.tensor_scalar_mul(out=graph[:, j, :], in0=graph[:, j, :], scalar1=dis[:, j : j + 1])
+            nc.scalar.activation(out=graph[:, j, :], in_=graph[:, j, :], func=ACT.Copy, scale=dis[:, j : j + 1])
         s_grouped = setup.tile([P, N, PACK], BF16, align_bytes=64)
         for vb in range(N_BLOCKS):
             v_cols = slice(vb * P, (vb + 1) * P)
@@ -134,7 +128,6 @@ def tile_dynamicgraphspatialconv_pb_t_kernel(tc, x, adj_param, tx1, cheb01, w_ch
         work = pools.enter_context(tc.tile_pool(name="work", bufs=2))
 
         ident_bf = keep.tile([P, P], BF16)
-        make_identity(nc, ident_bf[:])
         s_codes = keep.tile([P, N], U32, align_bytes=64)
         s_scales = keep.tile([P, N], U8, align_bytes=64)
         w_codes = keep.tile([P, C_OUT], U32, align_bytes=64)
@@ -256,14 +249,30 @@ def tile_dynamicgraphspatialconv_pb_t_kernel(tc, x, adj_param, tx1, cheb01, w_ch
             if quad == 0:
                 out_block = out_pool.tile([P, P, T], F32)
                 out_blocks[(b, vb)] = out_block
-            nc.vector.scalar_tensor_tensor(
-                out=out_blocks[(b, vb)][:, :, quad * QUAD : (quad + 1) * QUAD],
-                in0=unit_mixed[u][:].rearrange("o i v -> o v i"),
-                scalar=bias_col[:, 0:1],
-                in1=unit_cheb_t[u][:].rearrange("o i v -> o v i"),
-                op0=ALU.add,
-                op1=ALU.add,
-            )
+            out_steps = out_blocks[(b, vb)][:, :, quad * QUAD : (quad + 1) * QUAD]
+            if u % 2 == 1:
+                nc.vector.scalar_tensor_tensor(
+                    out=out_steps,
+                    in0=unit_mixed[u][:].rearrange("o i v -> o v i"),
+                    scalar=bias_col[:, 0:1],
+                    in1=unit_cheb_t[u][:].rearrange("o i v -> o v i"),
+                    op0=ALU.add,
+                    op1=ALU.add,
+                )
+            else:
+                biased = work.tile([P, P, QUAD], F32)
+                nc.scalar.activation(
+                    out=biased[:],
+                    in_=unit_mixed[u][:].rearrange("o i v -> o v i"),
+                    func=ACT.Identity,
+                    bias=bias_col[:, 0:1],
+                )
+                nc.gpsimd.tensor_tensor(
+                    out=out_steps,
+                    in0=biased[:],
+                    in1=unit_cheb_t[u][:].rearrange("o i v -> o v i"),
+                    op=ALU.add,
+                )
             if quad == N_QUADS - 1:
                 nc.sync.dma_start(out=out[b, :, vb * P : (vb + 1) * P, :], in_=out_blocks[(b, vb)][:])
 

@@ -24,12 +24,12 @@ N_UNITS = len(UNITS)
 N_STEPS = B * T
 assert N_BLOCKS == QUAD and N_UNITS == N_STEPS
 
-STEP_LOAD_AHEAD = 10
-STEP_REGROUP_AHEAD = 6
-STEP_QUANTISE_AHEAD = 5
-UNIT_LOAD_AHEAD = 6
+STEP_LOAD_AHEAD = 9
+STEP_REGROUP_AHEAD = 5
+STEP_QUANTISE_AHEAD = 4
+UNIT_LOAD_AHEAD = 5
 UNIT_MOVE_AHEAD = 2
-VECTOR_REGROUPS = QUAD
+SCALAR_COLS = 384
 
 FLOPS = 2 * B * T * N * N * C_IN + 2 * B * T * N * C_IN * C_OUT
 
@@ -38,122 +38,39 @@ def quantise(nc, codes, scales, grouped):
     nc.vector.quantize_mx(out=codes.bitcast(FP8X4), scales=scales, in_=grouped)
 
 
-def build_constants(tc, nc, banks, ident_bf, adj_param, w_cheb2, cheb_bias, s_codes, s_scales, w_codes, w_scales, bias_col):
-    with tc.tile_pool(name="setup", bufs=1) as setup:
-        adj_rows = setup.tile([P, PACK, N], BF16)
-        nc.sync.dma_start(out=adj_rows[:], in_=adj_param.rearrange("(p j) w -> p j w", j=PACK))
-        w_rows = setup.tile([P, PACK, C_OUT], BF16)
-        nc.sync.dma_start(out=w_rows[:], in_=w_cheb2.rearrange("(k p) o -> p k o", p=P))
-        bias_rows = setup.tile([P, P], BF16)
-        nc.vector.memset(bias_rows[:], 0.0)
-        nc.sync.dma_start(out=bias_rows[0:1, :], in_=cheb_bias.rearrange("(r o) -> r o", r=1))
-
-        ident_f32 = setup.tile([P, P], F32)
-        make_identity(nc, ident_f32[:])
-        make_identity(nc, ident_bf[:])
-
-        sig = setup.tile([P, PACK, PACK, P], F32)
-        sig_t = []
-        for cls in range(PACK):
-            nc.scalar.activation(
-                out=sig[:, cls, :, :],
-                in_=adj_rows[:].rearrange("q jj (m cls) -> q cls jj m", cls=PACK)[:, cls, :, :],
-                func=ACT.Sigmoid,
-            )
-            nc.gpsimd.affine_select(
-                out=sig[:, cls, :, :],
-                in_=sig[:, cls, :, :],
-                compare_op=ALU.not_equal,
-                fill=0.0,
-                base=-cls,
-                pattern=[[1, PACK], [-PACK, P]],
-                channel_multiplier=PACK,
-            )
-            sig_t_rows = banks.tile([P, PACK, P], F32, tag="first", bufs=QUAD)
-            for jj in range(PACK):
-                nc.tensor.transpose(sig_t_rows[:, jj, :], sig[:, cls, jj, :], ident_f32[:])
-            sig_t.append(sig_t_rows)
-
-        graph = setup.tile([P, PACK, N], F32)
-        row_sum = setup.tile([P, PACK], F32)
-        for j in range(PACK):
-            nc.vector.scalar_tensor_tensor(
-                out=graph[:, j, :].rearrange("p (m cls) -> p m cls", cls=PACK),
-                in0=sig[:, :, j, :].rearrange("p cls m -> p m cls"),
-                scalar=1.0,
-                in1=sig_t[j][:].rearrange("p cls m -> p m cls"),
-                op0=ALU.mult,
-                op1=ALU.add,
-                accum_out=row_sum[:, j : j + 1],
-            )
-        root = setup.tile([P, PACK], F32)
-        nc.scalar.activation(out=root[:, 0:1], in_=sig[:, PACK - 1, 0, 0:1], func=ACT.Sqrt)
-
-        nc.scalar.activation(out=root[:], in_=row_sum[:], func=ACT.Sqrt, scale=0.5)
-        dis = setup.tile([P, PACK], F32)
-        nc.vector.reciprocal(out=dis[:], in_=root[:])
-        repeated = setup.tile([P, PACK, P], F32)
-        nc.vector.tensor_scalar_mul(out=repeated[:], in0=dis[:].unsqueeze(2).to_broadcast([P, PACK, P]), scalar1=-0.5)
-        col_factor = banks.tile([P, PACK, P], F32, tag="small")
-        for jj in range(PACK):
-            nc.tensor.transpose(col_factor[:, jj, :], repeated[:, jj, :], ident_f32[:])
-        for j in range(PACK):
-            nc.scalar.activation(out=graph[:, j, :], in_=graph[:, j, :], func=ACT.Copy, scale=dis[:, j : j + 1])
-        s_grouped = setup.tile([P, N, PACK], BF16, align_bytes=64)
-        for vb in range(N_BLOCKS):
-            v_cols = slice(vb * P, (vb + 1) * P)
-            q_cols = slice(vb * P // PACK, (vb + 1) * P // PACK)
-            nc.vector.tensor_tensor(
-                out=s_grouped[:, v_cols, :].rearrange("p (q jj) j -> p q jj j", jj=PACK),
-                in0=graph[:, :, v_cols].rearrange("p j (q jj) -> p q jj j", jj=PACK),
-                in1=col_factor[:, :, q_cols].rearrange("p jj q -> p q jj").unsqueeze(3).to_broadcast([P, P // PACK, PACK, PACK]),
-                op=ALU.mult,
-            )
-            quantise(nc, s_codes[:, v_cols], s_scales[:, v_cols], s_grouped[:, v_cols, :].rearrange("p v j -> p (v j)"))
-
-        w_grouped = setup.tile([P, C_OUT, PACK], BF16, align_bytes=64)
-        nc.vector.tensor_copy(out=w_grouped[:], in_=w_rows[:].rearrange("p k o -> p o k"))
-        quantise(nc, w_codes[:], w_scales[:], w_grouped[:].rearrange("p o k -> p (o k)"))
-
-        bias_t = banks.tile([P, P], BF16, tag="small")
-        nc.tensor.transpose(bias_t[:], bias_rows[:], ident_bf[:])
-        nc.vector.tensor_copy(out=bias_col[:], in_=bias_t[:, 0:1])
-
-
 def tile_dynamicgraphspatialconv_pb_t_kernel(tc, x, adj_param, tx1, cheb01, w_cheb2, cheb_bias, out):
     nc = tc.nc
     with ExitStack() as pools:
         keep = pools.enter_context(tc.tile_pool(name="keep", bufs=1))
         banks = pools.enter_context(tc.psum_pool(name="banks", bufs=2))
         work = pools.enter_context(tc.tile_pool(name="work", bufs=2))
+        pools.enter_context(tc.manual_schedule())
 
+        ident_f32 = keep.tile([P, P], F32)
         ident_bf = keep.tile([P, P], BF16)
         s_codes = keep.tile([P, N], U32, align_bytes=64)
         s_scales = keep.tile([P, N], U8, align_bytes=64)
         w_codes = keep.tile([P, C_OUT], U32, align_bytes=64)
         w_scales = keep.tile([P, C_OUT], U8, align_bytes=64)
         bias_col = keep.tile([P, 1], F32)
-        build_constants(tc, nc, banks, ident_bf, adj_param, w_cheb2, cheb_bias, s_codes, s_scales, w_codes, w_scales, bias_col)
-
-        out_pool = pools.enter_context(tc.tile_pool(name="out", bufs=N_BLOCKS + 2))
 
         step_rows, step_grouped, quad_codes, quad_scales = {}, {}, {}, {}
-        unit_cheb_rows, unit_cheb_t, unit_x_quad, unit_products, unit_grouped, unit_mixed = {}, {}, {}, {}, {}, {}
+        unit_cheb_rows, unit_cheb_t, unit_x_quad, unit_products, unit_grouped, unit_mixed, unit_biased = {}, {}, {}, {}, {}, {}, {}
         x_blocks, out_blocks = {}, {}
 
         def load_step(s):
-            tx1_rows = work.tile([P, PACK, C_IN], BF16, bufs=STEP_LOAD_AHEAD - STEP_REGROUP_AHEAD + 2)
+            tx1_rows = work.tile([P, PACK, C_IN], BF16, bufs=6)
             nc.sync.dma_start(out=tx1_rows[:], in_=tx1[s // T, s % T].rearrange("(p j) c -> p j c", j=PACK))
             step_rows[s] = tx1_rows
 
-        def regroup_step(s):
-            tx1_grouped = work.tile([P, C_IN, PACK], BF16, bufs=STEP_REGROUP_AHEAD - STEP_QUANTISE_AHEAD + 2, align_bytes=64)
-            grouped_view = tx1_grouped[:].rearrange("p (c r) j -> p c j r", r=4)
-            rows_view = step_rows[s][:].rearrange("p j (c r) -> p c j r", r=4)
-            if s < VECTOR_REGROUPS:
-                nc.vector.tensor_copy(out=grouped_view, in_=rows_view)
-            else:
-                nc.scalar.copy(out=grouped_view, in_=rows_view)
+        def regroup(engine_copy, s, cols):
+            engine_copy(
+                out=step_grouped[s][:, cols, :].rearrange("p (c r) j -> p c j r", r=4),
+                in_=step_rows[s][:, :, cols].rearrange("p j (c r) -> p c j r", r=4),
+            )
+
+        def new_grouped(s):
+            tx1_grouped = work.tile([P, C_IN, PACK], BF16, bufs=4, align_bytes=64)
             step_grouped[s] = tx1_grouped
 
         def quantise_step(s):
@@ -164,30 +81,36 @@ def tile_dynamicgraphspatialconv_pb_t_kernel(tc, x, adj_param, tx1, cheb01, w_ch
                 quad_codes[g], quad_scales[g] = tx1_codes, tx1_scales
             quantise(nc, quad_codes[g][:, i, :], quad_scales[g][:, i, :], step_grouped[s][:].rearrange("p c j -> p (c j)"))
 
-        def load_unit(u):
+        def load_x(b, vb):
+            x_block = work.tile([P, PACK, P * T], BF16, bufs=N_BLOCKS + 1)
+            nc.sync.dma_start(
+                out=x_block[:],
+                in_=x[b].rearrange("(k p) v t -> p k (v t)", p=P)[:, :, vb * P * T : (vb + 1) * P * T],
+            )
+            x_blocks[(b, vb)] = x_block
+
+        def load_cheb(u):
             b, quad, vb = UNITS[u]
-            if quad == 0:
-                x_block = work.tile([P, PACK, P * T], BF16, bufs=N_BLOCKS + 2)
-                nc.sync.dma_start(
-                    out=x_block[:],
-                    in_=x[b].rearrange("(k p) v t -> p k (v t)", p=P)[:, :, vb * P * T : (vb + 1) * P * T],
-                )
-                x_blocks[(b, vb)] = x_block
-            cheb_rows = work.tile([P, QUAD, C_OUT], BF16, bufs=UNIT_LOAD_AHEAD - UNIT_MOVE_AHEAD + 2)
+            cheb_rows = work.tile([P, QUAD, C_OUT], BF16, bufs=6)
             nc.sync.dma_start(
                 out=cheb_rows[:],
                 in_=cheb01[b, quad * QUAD : (quad + 1) * QUAD, vb * P : (vb + 1) * P, :].rearrange("t v o -> v t o"),
             )
             unit_cheb_rows[u] = cheb_rows
 
-        def move_unit(u):
-            b, quad, vb = UNITS[u]
+        def turn_cheb(u):
             cheb_bank = banks.tile([P, QUAD, P], BF16, tag="turn")
             for i in range(QUAD):
                 nc.tensor.transpose(cheb_bank[:, i, :], unit_cheb_rows[u][:, i, :], ident_bf[:])
-            cheb_t = work.tile([P, QUAD, P], BF16, bufs=UNIT_MOVE_AHEAD + 3)
+            return cheb_bank
+
+        def keep_cheb(u, cheb_bank):
+            cheb_t = work.tile([P, QUAD, P], BF16, bufs=UNIT_MOVE_AHEAD + 4)
             nc.scalar.copy(out=cheb_t[:], in_=cheb_bank[:])
             unit_cheb_t[u] = cheb_t
+
+        def move_x(u):
+            b, quad, vb = UNITS[u]
             x_quad = work.tile([P, P, PACK, QUAD], BF16, bufs=UNIT_MOVE_AHEAD + 2)
             nc.scalar.copy(
                 out=x_quad[:].bitcast(F32),
@@ -244,61 +167,247 @@ def tile_dynamicgraphspatialconv_pb_t_kernel(tc, x, adj_param, tx1, cheb01, w_ch
             )
             unit_mixed[u] = mixed
 
-        def finish_unit(u):
+        def bias_unit(u):
+            biased = work.tile([P, P, QUAD], F32, bufs=3)
+            nc.scalar.activation(
+                out=biased[:],
+                in_=unit_mixed[u][:].rearrange("o i v -> o v i"),
+                func=ACT.Identity,
+                bias=bias_col[:, 0:1],
+            )
+            unit_biased[u] = biased
+
+        def out_steps_of(u):
             b, quad, vb = UNITS[u]
             if quad == 0:
                 out_block = out_pool.tile([P, P, T], F32)
                 out_blocks[(b, vb)] = out_block
-            out_steps = out_blocks[(b, vb)][:, :, quad * QUAD : (quad + 1) * QUAD]
-            if u % 2 == 1:
-                nc.vector.scalar_tensor_tensor(
-                    out=out_steps,
-                    in0=unit_mixed[u][:].rearrange("o i v -> o v i"),
-                    scalar=bias_col[:, 0:1],
-                    in1=unit_cheb_t[u][:].rearrange("o i v -> o v i"),
-                    op0=ALU.add,
-                    op1=ALU.add,
-                )
-            else:
-                biased = work.tile([P, P, QUAD], F32)
-                nc.scalar.activation(
-                    out=biased[:],
-                    in_=unit_mixed[u][:].rearrange("o i v -> o v i"),
-                    func=ACT.Identity,
-                    bias=bias_col[:, 0:1],
-                )
-                nc.gpsimd.tensor_tensor(
-                    out=out_steps,
-                    in0=biased[:],
-                    in1=unit_cheb_t[u][:].rearrange("o i v -> o v i"),
-                    op=ALU.add,
-                )
+            return out_blocks[(b, vb)][:, :, quad * QUAD : (quad + 1) * QUAD]
+
+        def add_cheb(u, gate_u):
+            gate = work.tile([P, 2], BF16)
+            nc.gpsimd.tensor_copy(out=gate[:], in_=unit_grouped[gate_u][:, 0, 0, 0:2])
+            nc.gpsimd.tensor_tensor(
+                out=out_steps_of(u),
+                in0=unit_biased[u][:],
+                in1=unit_cheb_t[u][:].rearrange("o i v -> o v i"),
+                op=ALU.add,
+            )
+
+        def finish_on_vector(u):
+            nc.vector.scalar_tensor_tensor(
+                out=out_steps_of(u),
+                in0=unit_mixed[u][:].rearrange("o i v -> o v i"),
+                scalar=bias_col[:, 0:1],
+                in1=unit_cheb_t[u][:].rearrange("o i v -> o v i"),
+                op0=ALU.add,
+                op1=ALU.add,
+            )
+
+        def store_unit(u):
+            b, quad, vb = UNITS[u]
             if quad == N_QUADS - 1:
                 nc.sync.dma_start(out=out[b, :, vb * P : (vb + 1) * P, :], in_=out_blocks[(b, vb)][:])
 
-        def run_round(u):
-            if 0 <= u + STEP_LOAD_AHEAD < N_STEPS:
-                load_step(u + STEP_LOAD_AHEAD)
-            if 0 <= u + UNIT_LOAD_AHEAD < N_UNITS:
-                load_unit(u + UNIT_LOAD_AHEAD)
-            if 0 <= u + STEP_REGROUP_AHEAD < N_STEPS:
-                regroup_step(u + STEP_REGROUP_AHEAD)
-            if 0 <= u + UNIT_MOVE_AHEAD < N_UNITS:
-                move_unit(u + UNIT_MOVE_AHEAD)
-            for i in range(QUAD):
-                if 0 <= u < N_UNITS:
-                    subtract_x(u, i)
-                if 0 <= u + 1 < N_UNITS:
-                    first_matmul(u + 1, i)
-            if 0 <= u + STEP_QUANTISE_AHEAD < N_STEPS:
-                quantise_step(u + STEP_QUANTISE_AHEAD)
-            if 0 <= u < N_UNITS:
-                second_matmul(u)
-            if 0 <= u - 1 < N_UNITS:
-                finish_unit(u - 1)
+        setup = pools.enter_context(tc.tile_pool(name="setup", bufs=1))
+        adj_rows = setup.tile([P, PACK, N], BF16)
+        nc.sync.dma_start(out=adj_rows[:], in_=adj_param.rearrange("(p j) w -> p j w", j=PACK))
+        for s in range(QUAD):
+            load_step(s)
+        load_x(0, 0)
+        w_rows = setup.tile([P, PACK, C_OUT], BF16)
+        nc.sync.dma_start(out=w_rows[:], in_=w_cheb2.rearrange("(k p) o -> p k o", p=P))
+        bias_rows = setup.tile([P, P], BF16)
+        nc.vector.memset(bias_rows[:], 0.0)
+        nc.sync.dma_start(out=bias_rows[0:1, :], in_=cheb_bias.rearrange("(r o) -> r o", r=1))
+        load_cheb(0)
+        load_step(4)
+        load_cheb(1)
+        load_x(0, 1)
+        load_cheb(2)
+        load_cheb(3)
+        load_x(0, 2)
+        load_step(5)
+        load_x(0, 3)
+        load_step(6)
+        load_step(7)
+        load_cheb(4)
+        load_step(8)
 
-        for u in range(-STEP_LOAD_AHEAD, 0):
+        make_identity(nc, ident_f32[:])
+        make_identity(nc, ident_bf[:])
+        power = setup.tile([P, PACK], F32)
+        nc.gpsimd.memset(power[:], -0.5)
+
+        new_grouped(0)
+        regroup(nc.vector.tensor_copy, 0, slice(0, C_IN))
+        quantise_step(0)
+
+        sig = setup.tile([P, PACK, PACK, P], F32)
+        sig_t = []
+        for cls in range(PACK):
+            nc.scalar.activation(
+                out=sig[:, cls, :, :],
+                in_=adj_rows[:].rearrange("q jj (m cls) -> q cls jj m", cls=PACK)[:, cls, :, :],
+                func=ACT.Sigmoid,
+            )
+            nc.gpsimd.affine_select(
+                out=sig[:, cls, cls, :],
+                in_=sig[:, cls, cls, :],
+                compare_op=ALU.not_equal,
+                fill=0.0,
+                base=0,
+                pattern=[[-1, P]],
+                channel_multiplier=1,
+            )
+            sig_t_rows = banks.tile([P, PACK, P], F32, tag="first", bufs=QUAD)
+            for jj in range(PACK):
+                nc.tensor.transpose(sig_t_rows[:, jj, :], sig[:, cls, jj, :], ident_f32[:])
+            sig_t.append(sig_t_rows)
+
+        new_grouped(1)
+        regroup(nc.scalar.copy, 1, slice(0, C_IN))
+        new_grouped(2)
+        regroup(nc.scalar.copy, 2, slice(0, C_IN))
+
+        graph = setup.tile([P, PACK, N], F32)
+        row_sum = setup.tile([P, PACK], F32)
+        for j in range(PACK):
+            nc.vector.scalar_tensor_tensor(
+                out=graph[:, j, :].rearrange("p (m cls) -> p m cls", cls=PACK),
+                in0=sig[:, :, j, :].rearrange("p cls m -> p m cls"),
+                scalar=1.0,
+                in1=sig_t[j][:].rearrange("p cls m -> p m cls"),
+                op0=ALU.mult,
+                op1=ALU.add,
+                accum_out=row_sum[:, j : j + 1],
+            )
+        dis = setup.tile([P, PACK], F32)
+        nc.gpsimd.tensor_tensor(out=dis[:], in0=row_sum[:], in1=power[:], op=ALU.pow)
+        quantise_step(1)
+        repeated = setup.tile([P, PACK, P], F32)
+        nc.vector.tensor_scalar_mul(out=repeated[:], in0=dis[:].unsqueeze(2).to_broadcast([P, PACK, P]), scalar1=-1.0)
+        col_factor = banks.tile([P, PACK, P], F32, tag="small")
+        for jj in range(PACK):
+            nc.tensor.transpose(col_factor[:, jj, :], repeated[:, jj, :], ident_f32[:])
+        for v_cols in (slice(0, P), slice(P, N)):
+            for j in range(PACK):
+                nc.gpsimd.tensor_scalar(
+                    out=graph[:, j, v_cols],
+                    in0=graph[:, j, v_cols],
+                    scalar1=dis[:, j : j + 1],
+                    scalar2=0.0,
+                    op0=ALU.mult,
+                    op1=ALU.add,
+                )
+        move_x(0)
+        col_later = setup.tile([P, PACK, P - P // PACK], F32)
+
+        s_grouped = setup.tile([P, N, PACK], BF16, align_bytes=64)
+
+        def quantise_s(vb):
+            v_cols = slice(vb * P, (vb + 1) * P)
+            q_cols = slice((vb - 1) * P // PACK, vb * P // PACK)
+            factor = col_factor[:, :, 0 : P // PACK] if vb == 0 else col_later[:, :, q_cols]
+            nc.vector.tensor_tensor(
+                out=s_grouped[:, v_cols, :].rearrange("p (q jj) j -> p q jj j", jj=PACK),
+                in0=graph[:, :, v_cols].rearrange("p j (q jj) -> p q jj j", jj=PACK),
+                in1=factor.rearrange("p jj q -> p q jj").unsqueeze(3).to_broadcast([P, P // PACK, PACK, PACK]),
+                op=ALU.mult,
+            )
+            quantise(nc, s_codes[:, v_cols], s_scales[:, v_cols], s_grouped[:, v_cols, :].rearrange("p v j -> p (v j)"))
+
+        new_grouped(3)
+        regroup(nc.vector.tensor_copy, 3, slice(0, C_IN))
+        quantise_s(0)
+        first_matmul(0, 0)
+        first_matmul(0, 1)
+        quantise_step(2)
+        first_matmul(0, 2)
+        quantise_step(3)
+        first_matmul(0, 3)
+        nc.scalar.copy(out=col_later[:], in_=col_factor[:, :, P // PACK :])
+        new_grouped(4)
+        regroup(nc.scalar.copy, 4, slice(0, C_IN))
+        keep_cheb(0, turn_cheb(0))
+        bias_t = banks.tile([P, P], BF16, tag="turn")
+        nc.tensor.transpose(bias_t[:], bias_rows[:], ident_bf[:])
+        nc.scalar.copy(out=bias_col[:], in_=bias_t[:, 0:1])
+        cheb_banks = {1: turn_cheb(1)}
+
+        out_pool = pools.enter_context(tc.tile_pool(name="out", bufs=N_BLOCKS))
+
+        def quantise_w():
+            w_grouped = setup.tile([P, C_OUT, PACK], BF16, align_bytes=64)
+            nc.vector.tensor_copy(out=w_grouped[:], in_=w_rows[:].rearrange("p k o -> p o k"))
+            quantise(nc, w_codes[:], w_scales[:], w_grouped[:].rearrange("p o k -> p (o k)"))
+
+        regroup_round = {s: s - 5 for s in range(9, N_STEPS)}
+        regroup_round.update({5: 2, 6: 3, 7: 3, 8: 3, 9: 4})
+        quantise_round = {s: s - 4 for s in range(8, N_STEPS)}
+        quantise_round.update({4: 1, 5: 3, 6: 3})
+
+        def regroup_step(s):
+            new_grouped(s)
+            cols = 256 if 5 <= s < 8 else SCALAR_COLS
+            regroup(nc.scalar.copy, s, slice(0, cols))
+            if cols < C_IN:
+                regroup(nc.vector.tensor_copy, s, slice(cols, C_IN))
+
+        def run_round(u):
+            if u + STEP_LOAD_AHEAD < N_STEPS:
+                load_step(u + STEP_LOAD_AHEAD)
+            if u + UNIT_LOAD_AHEAD < N_UNITS:
+                b, quad, vb = UNITS[u + UNIT_LOAD_AHEAD]
+                if quad == 0:
+                    load_x(b, vb)
+                load_cheb(u + UNIT_LOAD_AHEAD)
+            last = u == N_UNITS - 1
+            start = u < N_BLOCKS
+            if not start and u + 1 < N_UNITS:
+                move_x(u + 1)
+            for i in range(QUAD):
+                subtract_x(u, i)
+                if i == 0 and u >= 2:
+                    add_cheb(u - 2, u)
+                    store_unit(u - 2)
+                if u == N_BLOCKS and i == 1:
+                    quantise_step(7)
+                    first_matmul(4, 3)
+                if N_BLOCKS < u + 1 < N_UNITS and i < QUAD - 1:
+                    first_matmul(u + 1, i)
+            for s in regroup_round:
+                if regroup_round[s] == u:
+                    regroup_step(s)
+            if start:
+                move_x(u + 1)
+            if u + 1 in cheb_banks:
+                keep_cheb(u + 1, cheb_banks[u + 1])
+            if u >= 1 and not last:
+                bias_unit(u - 1)
+            if u + 1 < N_BLOCKS:
+                quantise_s(u + 1)
+            if u == 0:
+                quantise_w()
+            for s in quantise_round:
+                if quantise_round[s] == u:
+                    quantise_step(s)
+            if last:
+                after_gpsimd = work.tile([P, 2, 2], F32)
+                for i in range(2):
+                    nc.vector.tensor_copy(out=after_gpsimd[:, i, :], in_=out_blocks[(B - 1, N_BLOCKS - 2 + i)][:, 0, 0 : 2 * QUAD : QUAD])
+                finish_on_vector(u - 1)
+                store_unit(u - 1)
+            if u + 1 < N_UNITS:
+                for i in range(0 if u + 1 <= N_BLOCKS else QUAD - 1, QUAD):
+                    if (u + 1, i) != (4, 3):
+                        first_matmul(u + 1, i)
+            if u + 2 < N_UNITS:
+                cheb_banks[u + 2] = turn_cheb(u + 2)
+            second_matmul(u)
+            if last:
+                finish_on_vector(u)
+                store_unit(u)
+
+        for u in range(N_UNITS):
             run_round(u)
-        with tc.manual_schedule():
-            for u in range(0, N_UNITS + 1):
-                run_round(u)

@@ -186,7 +186,7 @@ def tile_dynamicgraphspatialconv_pb_t_kernel(tc, x, adj_param, tx1, cheb01, w_ch
 
         def add_cheb(u, gate_u):
             gate = work.tile([P, 2], BF16)
-            nc.gpsimd.tensor_copy(out=gate[:], in_=unit_grouped[gate_u][:, 0, 0, 0:2])
+            nc.gpsimd.tensor_tensor(out=gate[:], in0=unit_grouped[gate_u][:, 0, 0, 0:2], in1=unit_grouped[gate_u][:, 0, 0, 2:4], op=ALU.add)
             nc.gpsimd.tensor_tensor(
                 out=out_steps_of(u),
                 in0=unit_biased[u][:],
@@ -236,8 +236,6 @@ def tile_dynamicgraphspatialconv_pb_t_kernel(tc, x, adj_param, tx1, cheb01, w_ch
 
         make_identity(nc, ident_f32[:])
         make_identity(nc, ident_bf[:])
-        power = setup.tile([P, PACK], F32)
-        nc.gpsimd.memset(power[:], -0.5)
 
         new_grouped(0)
         regroup(nc.vector.tensor_copy, 0, slice(0, C_IN))
@@ -265,8 +263,10 @@ def tile_dynamicgraphspatialconv_pb_t_kernel(tc, x, adj_param, tx1, cheb01, w_ch
                 nc.tensor.transpose(sig_t_rows[:, jj, :], sig[:, cls, jj, :], ident_f32[:])
             sig_t.append(sig_t_rows)
 
+        root = setup.tile([P, PACK], F32)
+        nc.scalar.activation(out=root[:, 0:1], in_=sig[:, PACK - 1, 0, 0:1], func=ACT.Sqrt)
         new_grouped(1)
-        regroup(nc.scalar.copy, 1, slice(0, C_IN))
+        regroup(nc.vector.tensor_copy, 1, slice(0, C_IN))
         new_grouped(2)
         regroup(nc.scalar.copy, 2, slice(0, C_IN))
 
@@ -282,8 +282,9 @@ def tile_dynamicgraphspatialconv_pb_t_kernel(tc, x, adj_param, tx1, cheb01, w_ch
                 op1=ALU.add,
                 accum_out=row_sum[:, j : j + 1],
             )
+        nc.scalar.activation(out=root[:], in_=row_sum[:], func=ACT.Sqrt)
         dis = setup.tile([P, PACK], F32)
-        nc.gpsimd.tensor_tensor(out=dis[:], in0=row_sum[:], in1=power[:], op=ALU.pow)
+        nc.vector.reciprocal(out=dis[:], in_=root[:])
         quantise_step(1)
         repeated = setup.tile([P, PACK, P], F32)
         nc.vector.tensor_scalar_mul(out=repeated[:], in0=dis[:].unsqueeze(2).to_broadcast([P, PACK, P]), scalar1=-1.0)
@@ -292,14 +293,7 @@ def tile_dynamicgraphspatialconv_pb_t_kernel(tc, x, adj_param, tx1, cheb01, w_ch
             nc.tensor.transpose(col_factor[:, jj, :], repeated[:, jj, :], ident_f32[:])
         for v_cols in (slice(0, P), slice(P, N)):
             for j in range(PACK):
-                nc.gpsimd.tensor_scalar(
-                    out=graph[:, j, v_cols],
-                    in0=graph[:, j, v_cols],
-                    scalar1=dis[:, j : j + 1],
-                    scalar2=0.0,
-                    op0=ALU.mult,
-                    op1=ALU.add,
-                )
+                nc.scalar.activation(out=graph[:, j, v_cols], in_=graph[:, j, v_cols], func=ACT.Copy, scale=dis[:, j : j + 1])
         move_x(0)
         col_later = setup.tile([P, PACK, P - P // PACK], F32)
 

@@ -112,12 +112,12 @@ def tile_dynamicgraphspatialconv_pb_t_kernel(tc, x, adj_param, tx1, cheb01, w_ch
         def move_x(u):
             b, quad, vb = UNITS[u]
             x_quad = work.tile([P, P, PACK, QUAD], BF16, bufs=UNIT_MOVE_AHEAD + 2)
-            nc.scalar.copy(
-                out=x_quad[:].bitcast(F32),
-                in_=x_blocks[(b, vb)][:]
-                .bitcast(F32)
-                .rearrange("p k (v w) -> p v k w", w=T // 2)[:, :, :, quad * 2 : quad * 2 + 2],
-            )
+            x_words = x_blocks[(b, vb)][:].bitcast(F32).rearrange("p k (v w) -> p v k w", w=T // 2)
+            for k in range(0, PACK, 2):
+                nc.scalar.copy(
+                    out=x_quad[:, :, k : k + 2, :].bitcast(F32),
+                    in_=x_words[:, :, k : k + 2, quad * 2 : quad * 2 + 2],
+                )
             unit_x_quad[u] = x_quad
 
         def first_matmul(u, i):

@@ -15,21 +15,21 @@ B, C_IN, C_OUT, N, T = 2, 512, 128, 512, 12
 P = 128
 PACK = 4
 QUAD = 4
+PAIR = 2
 N_QUADS = T // QUAD
 N_BLOCKS = N // P
+HALF = P // 2
 assert C_IN == P * PACK and N == P * PACK and C_OUT == P
 
 UNITS = [(b, quad, vb) for b in range(B) for quad in range(N_QUADS) for vb in range(N_BLOCKS)]
 N_UNITS = len(UNITS)
 N_STEPS = B * T
+LAST = N_UNITS - 1
 assert N_BLOCKS == QUAD and N_UNITS == N_STEPS
 
 STEP_LOAD_AHEAD = 9
-STEP_REGROUP_AHEAD = 5
-STEP_QUANTISE_AHEAD = 4
 UNIT_LOAD_AHEAD = 5
-UNIT_MOVE_AHEAD = 2
-SCALAR_COLS = 384
+SCALAR_COLS = 288
 
 FLOPS = 2 * B * T * N * N * C_IN + 2 * B * T * N * C_IN * C_OUT
 
@@ -44,6 +44,8 @@ def tile_dynamicgraphspatialconv_pb_t_kernel(tc, x, adj_param, tx1, cheb01, w_ch
         keep = pools.enter_context(tc.tile_pool(name="keep", bufs=1))
         banks = pools.enter_context(tc.psum_pool(name="banks", bufs=2))
         work = pools.enter_context(tc.tile_pool(name="work", bufs=2))
+        setup = pools.enter_context(tc.tile_pool(name="setup", bufs=1))
+        out_pool = pools.enter_context(tc.tile_pool(name="out", bufs=N_BLOCKS))
         pools.enter_context(tc.manual_schedule())
 
         ident_f32 = keep.tile([P, P], F32)
@@ -55,7 +57,8 @@ def tile_dynamicgraphspatialconv_pb_t_kernel(tc, x, adj_param, tx1, cheb01, w_ch
         bias_col = keep.tile([P, 1], F32)
 
         step_rows, step_grouped, quad_codes, quad_scales = {}, {}, {}, {}
-        unit_cheb_rows, unit_cheb_t, unit_x_quad, unit_products, unit_grouped, unit_mixed, unit_biased = {}, {}, {}, {}, {}, {}, {}
+        unit_cheb_rows, unit_cheb_bank, unit_cheb_t, unit_x_pairs, unit_products = {}, {}, {}, {}, {}
+        unit_grouped, unit_codes, unit_scales, unit_mixed, unit_biased = {}, {}, {}, {}, {}
         x_blocks, out_blocks = {}, {}
 
         def load_step(s):
@@ -63,15 +66,15 @@ def tile_dynamicgraphspatialconv_pb_t_kernel(tc, x, adj_param, tx1, cheb01, w_ch
             nc.sync.dma_start(out=tx1_rows[:], in_=tx1[s // T, s % T].rearrange("(p j) c -> p j c", j=PACK))
             step_rows[s] = tx1_rows
 
-        def regroup(engine_copy, s, cols):
-            engine_copy(
-                out=step_grouped[s][:, cols, :].rearrange("p (c r) j -> p c j r", r=4),
-                in_=step_rows[s][:, :, cols].rearrange("p j (c r) -> p c j r", r=4),
-            )
-
-        def new_grouped(s):
+        def regroup_step(s, scalar_cols):
             tx1_grouped = work.tile([P, C_IN, PACK], BF16, bufs=4, align_bytes=64)
             step_grouped[s] = tx1_grouped
+            for engine_copy, cols in ((nc.scalar.copy, slice(0, scalar_cols)), (nc.vector.tensor_copy, slice(scalar_cols, C_IN))):
+                if cols.stop > cols.start:
+                    engine_copy(
+                        out=tx1_grouped[:, cols, :].rearrange("p (c r) j -> p c j r", r=4),
+                        in_=step_rows[s][:, :, cols].rearrange("p j (c r) -> p c j r", r=4),
+                    )
 
         def quantise_step(s):
             g, i = s // QUAD, s % QUAD
@@ -89,6 +92,16 @@ def tile_dynamicgraphspatialconv_pb_t_kernel(tc, x, adj_param, tx1, cheb01, w_ch
             )
             x_blocks[(b, vb)] = x_block
 
+        def pair_x(u):
+            b, quad, vb = UNITS[u]
+            x_pairs = work.tile([P, QUAD // PAIR, P, PACK, PAIR], BF16, bufs=3)
+            x_words = x_blocks[(b, vb)][:].bitcast(F32).rearrange("p k (v w) -> p v k w", w=T // PAIR)
+            nc.scalar.copy(
+                out=x_pairs[:].bitcast(F32).rearrange("p w v k e -> p v k (w e)"),
+                in_=x_words[:, :, :, quad * QUAD // PAIR : (quad + 1) * QUAD // PAIR],
+            )
+            unit_x_pairs[u] = x_pairs
+
         def load_cheb(u):
             b, quad, vb = UNITS[u]
             cheb_rows = work.tile([P, QUAD, C_OUT], BF16, bufs=6)
@@ -102,23 +115,12 @@ def tile_dynamicgraphspatialconv_pb_t_kernel(tc, x, adj_param, tx1, cheb01, w_ch
             cheb_bank = banks.tile([P, QUAD, P], BF16, tag="turn")
             for i in range(QUAD):
                 nc.tensor.transpose(cheb_bank[:, i, :], unit_cheb_rows[u][:, i, :], ident_bf[:])
-            return cheb_bank
+            unit_cheb_bank[u] = cheb_bank
 
-        def keep_cheb(u, cheb_bank):
-            cheb_t = work.tile([P, QUAD, P], BF16, bufs=UNIT_MOVE_AHEAD + 4)
-            nc.scalar.copy(out=cheb_t[:], in_=cheb_bank[:])
+        def keep_cheb(u):
+            cheb_t = work.tile([P, QUAD, P], BF16, bufs=6)
+            nc.scalar.copy(out=cheb_t[:], in_=unit_cheb_bank[u][:])
             unit_cheb_t[u] = cheb_t
-
-        def move_x(u):
-            b, quad, vb = UNITS[u]
-            x_quad = work.tile([P, P, PACK, QUAD], BF16, bufs=UNIT_MOVE_AHEAD + 2)
-            x_words = x_blocks[(b, vb)][:].bitcast(F32).rearrange("p k (v w) -> p v k w", w=T // 2)
-            for k in range(0, PACK, 2):
-                nc.scalar.copy(
-                    out=x_quad[:, :, k : k + 2, :].bitcast(F32),
-                    in_=x_words[:, :, k : k + 2, quad * 2 : quad * 2 + 2],
-                )
-            unit_x_quad[u] = x_quad
 
         def first_matmul(u, i):
             vb = UNITS[u][2]
@@ -138,40 +140,51 @@ def tile_dynamicgraphspatialconv_pb_t_kernel(tc, x, adj_param, tx1, cheb01, w_ch
                 )
             unit_products[(u, i)] = product
 
-        def subtract_x(u, i):
-            if i == 0:
-                tx2_grouped = work.tile([P, QUAD, P, PACK], BF16, align_bytes=64)
+        def parts_of(u):
+            return [slice(0, HALF), slice(HALF, P)] if u == LAST else [slice(0, P)]
+
+        def part_columns(u, part):
+            return slice(part.start * QUAD, part.stop * QUAD)
+
+        def subtract_x(u, i, part):
+            if u not in unit_grouped:
+                tx2_grouped = work.tile([P, QUAD * P, PACK], BF16, align_bytes=64)
                 unit_grouped[u] = tx2_grouped
             nc.vector.scalar_tensor_tensor(
-                out=unit_grouped[u][:, i, :, :],
-                in0=unit_products[(u, i)][:].rearrange("p k v -> p v k"),
+                out=unit_grouped[u][:, part_columns(u, part), :].rearrange("p (i v) k -> p i v k", i=QUAD)[:, i, :, :],
+                in0=unit_products[(u, i)][:, :, part].rearrange("p k v -> p v k"),
                 scalar=2.0,
-                in1=unit_x_quad[u][:, :, :, i],
+                in1=unit_x_pairs[u][:, i // PAIR, part, :, i % PAIR],
                 op0=ALU.mult,
                 op1=ALU.subtract,
             )
 
-        def second_matmul(u):
-            tx2_codes = work.tile([P, QUAD * P], U32, align_bytes=64)
-            tx2_scales = work.tile([P, QUAD * P], U8, align_bytes=64)
-            quantise(nc, tx2_codes[:], tx2_scales[:], unit_grouped[u][:].rearrange("p i v k -> p (i v k)"))
-            mixed = banks.tile([P, QUAD, P], F32, tag="small")
+        def quantise_unit(u, part):
+            if u not in unit_codes:
+                tx2_codes = work.tile([P, QUAD * P], U32, align_bytes=64)
+                tx2_scales = work.tile([P, QUAD * P], U8, align_bytes=64)
+                mixed = banks.tile([P, QUAD * P], F32, tag="small")
+                unit_codes[u], unit_scales[u], unit_mixed[u] = tx2_codes, tx2_scales, mixed
+            cols = part_columns(u, part)
+            quantise(nc, unit_codes[u][:, cols], unit_scales[u][:, cols], unit_grouped[u][:, cols, :].rearrange("p n k -> p (n k)"))
+
+        def second_matmul(u, part):
+            cols = part_columns(u, part)
             nc.tensor.matmul_mx(
-                out=mixed[:].rearrange("o i v -> o (i v)"),
+                out=unit_mixed[u][:, cols],
                 lhsT=w_codes[:].bitcast(FP8X4),
                 lhsT_scale=w_scales[:],
-                rhs=tx2_codes[:].bitcast(FP8X4),
-                rhs_scale=tx2_scales[:],
+                rhs=unit_codes[u][:, cols].bitcast(FP8X4),
+                rhs_scale=unit_scales[u][:, cols],
                 start=True,
                 stop=True,
             )
-            unit_mixed[u] = mixed
 
         def bias_unit(u):
             biased = work.tile([P, P, QUAD], F32, bufs=3)
             nc.scalar.activation(
                 out=biased[:],
-                in_=unit_mixed[u][:].rearrange("o i v -> o v i"),
+                in_=unit_mixed[u][:].rearrange("o (i v) -> o v i", i=QUAD),
                 func=ACT.Identity,
                 bias=bias_col[:, 0:1],
             )
@@ -185,31 +198,34 @@ def tile_dynamicgraphspatialconv_pb_t_kernel(tc, x, adj_param, tx1, cheb01, w_ch
             return out_blocks[(b, vb)][:, :, quad * QUAD : (quad + 1) * QUAD]
 
         def add_cheb(u, gate_u):
-            gate = work.tile([P, 2], BF16)
-            nc.gpsimd.tensor_tensor(out=gate[:], in0=unit_grouped[gate_u][:, 0, 0, 0:2], in1=unit_grouped[gate_u][:, 0, 0, 2:4], op=ALU.add)
+            gate = work.tile([P, 1], U32)
+            nc.gpsimd.tensor_copy(out=gate[:], in_=unit_codes[gate_u][:, 0:1])
             nc.gpsimd.tensor_tensor(
                 out=out_steps_of(u),
                 in0=unit_biased[u][:],
                 in1=unit_cheb_t[u][:].rearrange("o i v -> o v i"),
                 op=ALU.add,
             )
+            store_part(u, slice(0, P))
 
-        def finish_on_vector(u):
+        def finish_on_vector(u, part):
             nc.vector.scalar_tensor_tensor(
-                out=out_steps_of(u),
-                in0=unit_mixed[u][:].rearrange("o i v -> o v i"),
+                out=out_steps_of(u)[:, part, :],
+                in0=unit_mixed[u][:, part_columns(u, part)].rearrange("o (i v) -> o v i", i=QUAD),
                 scalar=bias_col[:, 0:1],
-                in1=unit_cheb_t[u][:].rearrange("o i v -> o v i"),
+                in1=unit_cheb_t[u][:, :, part].rearrange("o i v -> o v i"),
                 op0=ALU.add,
                 op1=ALU.add,
             )
+            store_part(u, part)
 
-        def store_unit(u):
+        def store_part(u, part):
             b, quad, vb = UNITS[u]
             if quad == N_QUADS - 1:
-                nc.sync.dma_start(out=out[b, :, vb * P : (vb + 1) * P, :], in_=out_blocks[(b, vb)][:])
+                nc.sync.dma_start(
+                    out=out[b, :, vb * P + part.start : vb * P + part.stop, :], in_=out_blocks[(b, vb)][:, part, :]
+                )
 
-        setup = pools.enter_context(tc.tile_pool(name="setup", bufs=1))
         adj_rows = setup.tile([P, PACK, N], BF16)
         nc.sync.dma_start(out=adj_rows[:], in_=adj_param.rearrange("(p j) w -> p j w", j=PACK))
         for s in range(QUAD):
@@ -237,8 +253,7 @@ def tile_dynamicgraphspatialconv_pb_t_kernel(tc, x, adj_param, tx1, cheb01, w_ch
         make_identity(nc, ident_f32[:])
         make_identity(nc, ident_bf[:])
 
-        new_grouped(0)
-        regroup(nc.vector.tensor_copy, 0, slice(0, C_IN))
+        regroup_step(0, 0)
         quantise_step(0)
 
         sig = setup.tile([P, PACK, PACK, P], F32)
@@ -265,10 +280,8 @@ def tile_dynamicgraphspatialconv_pb_t_kernel(tc, x, adj_param, tx1, cheb01, w_ch
 
         root = setup.tile([P, PACK], F32)
         nc.scalar.activation(out=root[:, 0:1], in_=sig[:, PACK - 1, 0, 0:1], func=ACT.Sqrt)
-        new_grouped(1)
-        regroup(nc.vector.tensor_copy, 1, slice(0, C_IN))
-        new_grouped(2)
-        regroup(nc.scalar.copy, 2, slice(0, C_IN))
+        regroup_step(1, 0)
+        regroup_step(2, C_IN)
 
         graph = setup.tile([P, PACK, N], F32)
         row_sum = setup.tile([P, PACK], F32)
@@ -294,9 +307,8 @@ def tile_dynamicgraphspatialconv_pb_t_kernel(tc, x, adj_param, tx1, cheb01, w_ch
         for v_cols in (slice(0, P), slice(P, N)):
             for j in range(PACK):
                 nc.scalar.activation(out=graph[:, j, v_cols], in_=graph[:, j, v_cols], func=ACT.Copy, scale=dis[:, j : j + 1])
-        move_x(0)
+        pair_x(0)
         col_later = setup.tile([P, PACK, P - P // PACK], F32)
-
         s_grouped = setup.tile([P, N, PACK], BF16, align_bytes=64)
 
         def quantise_s(vb):
@@ -311,8 +323,12 @@ def tile_dynamicgraphspatialconv_pb_t_kernel(tc, x, adj_param, tx1, cheb01, w_ch
             )
             quantise(nc, s_codes[:, v_cols], s_scales[:, v_cols], s_grouped[:, v_cols, :].rearrange("p v j -> p (v j)"))
 
-        new_grouped(3)
-        regroup(nc.vector.tensor_copy, 3, slice(0, C_IN))
+        def quantise_w():
+            w_grouped = setup.tile([P, C_OUT, PACK], BF16, align_bytes=64)
+            nc.vector.tensor_copy(out=w_grouped[:], in_=w_rows[:].rearrange("p k o -> p o k"))
+            quantise(nc, w_codes[:], w_scales[:], w_grouped[:].rearrange("p o k -> p (o k)"))
+
+        regroup_step(3, 0)
         quantise_s(0)
         first_matmul(0, 0)
         first_matmul(0, 1)
@@ -321,32 +337,18 @@ def tile_dynamicgraphspatialconv_pb_t_kernel(tc, x, adj_param, tx1, cheb01, w_ch
         quantise_step(3)
         first_matmul(0, 3)
         nc.scalar.copy(out=col_later[:], in_=col_factor[:, :, P // PACK :])
-        new_grouped(4)
-        regroup(nc.scalar.copy, 4, slice(0, C_IN))
-        keep_cheb(0, turn_cheb(0))
+        regroup_step(4, C_IN)
+        turn_cheb(0)
+        keep_cheb(0)
         bias_t = banks.tile([P, P], BF16, tag="turn")
         nc.tensor.transpose(bias_t[:], bias_rows[:], ident_bf[:])
         nc.scalar.copy(out=bias_col[:], in_=bias_t[:, 0:1])
-        cheb_banks = {1: turn_cheb(1)}
+        turn_cheb(1)
 
-        out_pool = pools.enter_context(tc.tile_pool(name="out", bufs=N_BLOCKS))
-
-        def quantise_w():
-            w_grouped = setup.tile([P, C_OUT, PACK], BF16, align_bytes=64)
-            nc.vector.tensor_copy(out=w_grouped[:], in_=w_rows[:].rearrange("p k o -> p o k"))
-            quantise(nc, w_codes[:], w_scales[:], w_grouped[:].rearrange("p o k -> p (o k)"))
-
-        regroup_round = {s: s - 5 for s in range(9, N_STEPS)}
+        regroup_round = {s: s - 5 for s in range(10, N_STEPS)}
         regroup_round.update({5: 2, 6: 3, 7: 3, 8: 3, 9: 4})
         quantise_round = {s: s - 4 for s in range(8, N_STEPS)}
         quantise_round.update({4: 1, 5: 3, 6: 3})
-
-        def regroup_step(s):
-            new_grouped(s)
-            cols = 256 if 5 <= s < 8 else SCALAR_COLS
-            regroup(nc.scalar.copy, s, slice(0, cols))
-            if cols < C_IN:
-                regroup(nc.vector.tensor_copy, s, slice(cols, C_IN))
 
         def run_round(u):
             if u + STEP_LOAD_AHEAD < N_STEPS:
@@ -356,29 +358,38 @@ def tile_dynamicgraphspatialconv_pb_t_kernel(tc, x, adj_param, tx1, cheb01, w_ch
                 if quad == 0:
                     load_x(b, vb)
                 load_cheb(u + UNIT_LOAD_AHEAD)
-            last = u == N_UNITS - 1
             start = u < N_BLOCKS
-            if not start and u + 1 < N_UNITS:
-                move_x(u + 1)
-            for i in range(QUAD):
-                subtract_x(u, i)
-                if i == 0 and u >= 2:
-                    add_cheb(u - 2, u)
-                    store_unit(u - 2)
-                if u == N_BLOCKS and i == 1:
-                    quantise_step(7)
-                    first_matmul(4, 3)
-                if N_BLOCKS < u + 1 < N_UNITS and i < QUAD - 1:
-                    first_matmul(u + 1, i)
+            if not start and u < LAST:
+                pair_x(u + 1)
+            if 2 <= u < LAST:
+                add_cheb(u - 2, u - 1)
+            for part in parts_of(u):
+                for i in range(QUAD):
+                    subtract_x(u, i, part)
+                    if u == LAST and part.start == 0 and i == 1:
+                        after_gpsimd = work.tile([P, 2, 2], F32)
+                        for n in range(2):
+                            nc.vector.tensor_copy(out=after_gpsimd[:, n, :], in_=out_blocks[(B - 1, N_BLOCKS - 2 + n)][:, 0, 0 : 2 * QUAD : QUAD])
+                        finish_on_vector(u - 1, slice(0, P))
+                    if u == N_BLOCKS and i == 1:
+                        quantise_step(7)
+                        first_matmul(u, QUAD - 1)
+                    if N_BLOCKS < u + 1 < N_UNITS and i < QUAD - 1:
+                        first_matmul(u + 1, i)
+                if u == LAST and part.start == 0:
+                    quantise_unit(u, part)
+                    second_matmul(u, part)
             for s in regroup_round:
                 if regroup_round[s] == u:
-                    regroup_step(s)
+                    regroup_step(s, 256 if s < 2 * QUAD else SCALAR_COLS)
             if start:
-                move_x(u + 1)
-            if u + 1 in cheb_banks:
-                keep_cheb(u + 1, cheb_banks[u + 1])
-            if u >= 1 and not last:
+                pair_x(u + 1)
+            if u < LAST:
+                keep_cheb(u + 1)
+            if 1 <= u < LAST:
                 bias_unit(u - 1)
+            if u == LAST - 1:
+                add_cheb(u - 1, u - 1)
             if u + 1 < N_BLOCKS:
                 quantise_s(u + 1)
             if u == 0:
@@ -386,22 +397,19 @@ def tile_dynamicgraphspatialconv_pb_t_kernel(tc, x, adj_param, tx1, cheb01, w_ch
             for s in quantise_round:
                 if quantise_round[s] == u:
                     quantise_step(s)
-            if last:
-                after_gpsimd = work.tile([P, 2, 2], F32)
-                for i in range(2):
-                    nc.vector.tensor_copy(out=after_gpsimd[:, i, :], in_=out_blocks[(B - 1, N_BLOCKS - 2 + i)][:, 0, 0 : 2 * QUAD : QUAD])
-                finish_on_vector(u - 1)
-                store_unit(u - 1)
-            if u + 1 < N_UNITS:
+            if u < LAST:
                 for i in range(0 if u + 1 <= N_BLOCKS else QUAD - 1, QUAD):
-                    if (u + 1, i) != (4, 3):
+                    if (u + 1, i) != (N_BLOCKS, QUAD - 1):
                         first_matmul(u + 1, i)
             if u + 2 < N_UNITS:
-                cheb_banks[u + 2] = turn_cheb(u + 2)
-            second_matmul(u)
-            if last:
-                finish_on_vector(u)
-                store_unit(u)
+                turn_cheb(u + 2)
+            if u == LAST:
+                finish_on_vector(u, slice(0, HALF))
+            part = parts_of(u)[-1]
+            quantise_unit(u, part)
+            second_matmul(u, part)
+            if u == LAST:
+                finish_on_vector(u, part)
 
         for u in range(N_UNITS):
             run_round(u)

@@ -29,7 +29,6 @@ assert N_BLOCKS == QUAD and N_UNITS == N_STEPS
 
 STEP_LOAD_AHEAD = 9
 UNIT_LOAD_AHEAD = 5
-SCALAR_COLS = 288
 
 FLOPS = 2 * B * T * N * N * C_IN + 2 * B * T * N * C_IN * C_OUT
 
@@ -66,10 +65,23 @@ def tile_dynamicgraphspatialconv_pb_t_kernel(tc, x, adj_param, tx1, cheb01, w_ch
             nc.sync.dma_start(out=tx1_rows[:], in_=tx1[s // T, s % T].rearrange("(p j) c -> p j c", j=PACK))
             step_rows[s] = tx1_rows
 
-        def regroup_step(s, scalar_cols):
+        def regroup_step(s, scalar_cols, vector_cols):
             tx1_grouped = work.tile([P, C_IN, PACK], BF16, bufs=4, align_bytes=64)
             step_grouped[s] = tx1_grouped
-            for engine_copy, cols in ((nc.scalar.copy, slice(0, scalar_cols)), (nc.vector.tensor_copy, slice(scalar_cols, C_IN))):
+            gpsimd_cols = slice(scalar_cols + vector_cols, C_IN)
+            if gpsimd_cols.start < C_IN:
+                nc.gpsimd.tensor_scalar(
+                    out=tx1_grouped[:, gpsimd_cols, :],
+                    in0=step_rows[s][:, :, gpsimd_cols].rearrange("p j c -> p c j"),
+                    scalar1=1.0,
+                    scalar2=0.0,
+                    op0=ALU.mult,
+                    op1=ALU.add,
+                )
+            for engine_copy, cols in (
+                (nc.scalar.copy, slice(0, scalar_cols)),
+                (nc.vector.tensor_copy, slice(scalar_cols, gpsimd_cols.start)),
+            ):
                 if cols.stop > cols.start:
                     engine_copy(
                         out=tx1_grouped[:, cols, :].rearrange("p (c r) j -> p c j r", r=4),
@@ -197,9 +209,11 @@ def tile_dynamicgraphspatialconv_pb_t_kernel(tc, x, adj_param, tx1, cheb01, w_ch
                 out_blocks[(b, vb)] = out_block
             return out_blocks[(b, vb)][:, :, quad * QUAD : (quad + 1) * QUAD]
 
-        def add_cheb(u, gate_u):
+        def wait_on_gpsimd(u):
             gate = work.tile([P, 1], U32)
-            nc.gpsimd.tensor_copy(out=gate[:], in_=unit_codes[gate_u][:, 0:1])
+            nc.gpsimd.tensor_copy(out=gate[:], in_=unit_codes[u][:, 0:1])
+
+        def add_cheb(u):
             nc.gpsimd.tensor_tensor(
                 out=out_steps_of(u),
                 in0=unit_biased[u][:],
@@ -253,7 +267,7 @@ def tile_dynamicgraphspatialconv_pb_t_kernel(tc, x, adj_param, tx1, cheb01, w_ch
         make_identity(nc, ident_f32[:])
         make_identity(nc, ident_bf[:])
 
-        regroup_step(0, 0)
+        regroup_step(0, 0, C_IN)
         quantise_step(0)
 
         sig = setup.tile([P, PACK, PACK, P], F32)
@@ -280,8 +294,8 @@ def tile_dynamicgraphspatialconv_pb_t_kernel(tc, x, adj_param, tx1, cheb01, w_ch
 
         root = setup.tile([P, PACK], F32)
         nc.scalar.activation(out=root[:, 0:1], in_=sig[:, PACK - 1, 0, 0:1], func=ACT.Sqrt)
-        regroup_step(1, 0)
-        regroup_step(2, C_IN)
+        regroup_step(1, 0, C_IN)
+        regroup_step(2, C_IN, 0)
 
         graph = setup.tile([P, PACK, N], F32)
         row_sum = setup.tile([P, PACK], F32)
@@ -328,7 +342,7 @@ def tile_dynamicgraphspatialconv_pb_t_kernel(tc, x, adj_param, tx1, cheb01, w_ch
             nc.vector.tensor_copy(out=w_grouped[:], in_=w_rows[:].rearrange("p k o -> p o k"))
             quantise(nc, w_codes[:], w_scales[:], w_grouped[:].rearrange("p o k -> p (o k)"))
 
-        regroup_step(3, 0)
+        regroup_step(3, 0, C_IN)
         quantise_s(0)
         first_matmul(0, 0)
         first_matmul(0, 1)
@@ -337,7 +351,7 @@ def tile_dynamicgraphspatialconv_pb_t_kernel(tc, x, adj_param, tx1, cheb01, w_ch
         quantise_step(3)
         first_matmul(0, 3)
         nc.scalar.copy(out=col_later[:], in_=col_factor[:, :, P // PACK :])
-        regroup_step(4, C_IN)
+        regroup_step(4, C_IN, 0)
         turn_cheb(0)
         keep_cheb(0)
         bias_t = banks.tile([P, P], BF16, tag="turn")
@@ -362,14 +376,15 @@ def tile_dynamicgraphspatialconv_pb_t_kernel(tc, x, adj_param, tx1, cheb01, w_ch
             if not start and u < LAST:
                 pair_x(u + 1)
             if 2 <= u < LAST:
-                add_cheb(u - 2, u - 1)
+                wait_on_gpsimd(u - 1)
+            if 2 <= u < LAST and u % 2 == 0:
+                add_cheb(u - 2)
             for part in parts_of(u):
                 for i in range(QUAD):
                     subtract_x(u, i, part)
                     if u == LAST and part.start == 0 and i == 1:
-                        after_gpsimd = work.tile([P, 2, 2], F32)
-                        for n in range(2):
-                            nc.vector.tensor_copy(out=after_gpsimd[:, n, :], in_=out_blocks[(B - 1, N_BLOCKS - 2 + n)][:, 0, 0 : 2 * QUAD : QUAD])
+                        after_gpsimd = work.tile([P, 2], F32)
+                        nc.vector.tensor_copy(out=after_gpsimd[:], in_=out_blocks[(B - 1, N_BLOCKS - 2)][:, 0, 0 : 2 * QUAD : QUAD])
                         finish_on_vector(u - 1, slice(0, P))
                     if u == N_BLOCKS and i == 1:
                         quantise_step(7)
@@ -381,15 +396,15 @@ def tile_dynamicgraphspatialconv_pb_t_kernel(tc, x, adj_param, tx1, cheb01, w_ch
                     second_matmul(u, part)
             for s in regroup_round:
                 if regroup_round[s] == u:
-                    regroup_step(s, 256 if s < 2 * QUAD else SCALAR_COLS)
+                    regroup_step(s, *((192, 0) if s % 2 == 0 else (C_IN, 0) if s >= 2 * QUAD else (256, 256)))
             if start:
                 pair_x(u + 1)
             if u < LAST:
                 keep_cheb(u + 1)
-            if 1 <= u < LAST:
+            if 1 <= u < LAST and u % 2 == 1:
                 bias_unit(u - 1)
-            if u == LAST - 1:
-                add_cheb(u - 1, u - 1)
+            if 1 <= u < LAST and u % 2 == 0:
+                finish_on_vector(u - 1, slice(0, P))
             if u + 1 < N_BLOCKS:
                 quantise_s(u + 1)
             if u == 0:

from contextlib import ExitStack

import concourse.mybir as mybir
from concourse.masks import make_identity

F32 = mybir.dt.float32
BF16 = mybir.dt.bfloat16
U32 = mybir.dt.uint32
U8 = mybir.dt.uint8
FP8X4 = mybir.dt.float8_e4m3fn_x4
ALU = mybir.AluOpType
ACT = mybir.ActivationFunctionType

B, C_IN, C_OUT, N, T = 2, 512, 128, 512, 12
P = 128
PACK = 4
QUAD = 4
PAIR = 2
N_QUADS = T // QUAD
N_BLOCKS = N // P
HALF = P // 2
assert C_IN == P * PACK and N == P * PACK and C_OUT == P

UNITS = [(b, quad, vb) for b in range(B) for quad in range(N_QUADS) for vb in range(N_BLOCKS)]
N_UNITS = len(UNITS)
N_STEPS = B * T
LAST = N_UNITS - 1
assert N_BLOCKS == QUAD and N_UNITS == N_STEPS

STEP_LOAD_AHEAD = 9
UNIT_LOAD_AHEAD = 5

FLOPS = 2 * B * T * N * N * C_IN + 2 * B * T * N * C_IN * C_OUT


def quantise(nc, codes, scales, grouped):
    nc.vector.quantize_mx(out=codes.bitcast(FP8X4), scales=scales, in_=grouped)


def tile_dynamicgraphspatialconv_pb_t_kernel(tc, x, adj_param, tx1, cheb01, w_cheb2, cheb_bias, out):
    nc = tc.nc
    with ExitStack() as pools:
        keep = pools.enter_context(tc.tile_pool(name="keep", bufs=1))
        banks = pools.enter_context(tc.psum_pool(name="banks", bufs=2))
        work = pools.enter_context(tc.tile_pool(name="work", bufs=2))
        setup = pools.enter_context(tc.tile_pool(name="setup", bufs=1))
        out_pool = pools.enter_context(tc.tile_pool(name="out", bufs=N_BLOCKS))
        pools.enter_context(tc.manual_schedule())

        ident_f32 = keep.tile([P, P], F32)
        ident_bf = keep.tile([P, P], BF16)
        s_codes = keep.tile([P, N], U32, align_bytes=64)
        s_scales = keep.tile([P, N], U8, align_bytes=64)
        w_codes = keep.tile([P, C_OUT], U32, align_bytes=64)
        w_scales = keep.tile([P, C_OUT], U8, align_bytes=64)
        bias_col = keep.tile([P, 1], F32)

        step_rows, step_grouped, quad_codes, quad_scales = {}, {}, {}, {}
        unit_cheb_rows, unit_cheb_bank, unit_cheb_t, unit_x_pairs, unit_products = {}, {}, {}, {}, {}
        unit_grouped, unit_codes, unit_scales, unit_mixed, unit_biased = {}, {}, {}, {}, {}
        x_blocks, out_blocks = {}, {}

        def load_step(s):
            tx1_rows = work.tile([P, PACK, C_IN], BF16, bufs=6)
            nc.sync.dma_start(out=tx1_rows[:], in_=tx1[s // T, s % T].rearrange("(p j) c -> p j c", j=PACK))
            step_rows[s] = tx1_rows

        def regroup_step(s, scalar_cols, vector_cols):
            tx1_grouped = work.tile([P, C_IN, PACK], BF16, bufs=4, align_bytes=64)
            step_grouped[s] = tx1_grouped
            gpsimd_cols = slice(scalar_cols + vector_cols, C_IN)
            if gpsimd_cols.start < C_IN:
                nc.gpsimd.tensor_scalar(
                    out=tx1_grouped[:, gpsimd_cols, :],
                    in0=step_rows[s][:, :, gpsimd_cols].rearrange("p j c -> p c j"),
                    scalar1=1.0,
                    scalar2=0.0,
                    op0=ALU.mult,
                    op1=ALU.add,
                )
            for engine_copy, cols in (
                (nc.scalar.copy, slice(0, scalar_cols)),
                (nc.vector.tensor_copy, slice(scalar_cols, gpsimd_cols.start)),
            ):
                if cols.stop > cols.start:
                    engine_copy(
                        out=tx1_grouped[:, cols, :].rearrange("p (c r) j -> p c j r", r=4),
                        in_=step_rows[s][:, :, cols].rearrange("p j (c r) -> p c j r", r=4),
                    )

        def quantise_step(s):
            g, i = s // QUAD, s % QUAD
            if i == 0:
                tx1_codes = work.tile([P, QUAD, C_IN], U32, align_bytes=64)
                tx1_scales = work.tile([P, QUAD, C_IN], U8, align_bytes=64)
                quad_codes[g], quad_scales[g] = tx1_codes, tx1_scales
            quantise(nc, quad_codes[g][:, i, :], quad_scales[g][:, i, :], step_grouped[s][:].rearrange("p c j -> p (c j)"))

        def load_x(b, vb):
            x_block = work.tile([P, PACK, P * T], BF16, bufs=N_BLOCKS + 1)
            nc.sync.dma_start(
                out=x_block[:],
                in_=x[b].rearrange("(k p) v t -> p k (v t)", p=P)[:, :, vb * P * T : (vb + 1) * P * T],
            )
            x_blocks[(b, vb)] = x_block

        def pair_x(u):
            b, quad, vb = UNITS[u]
            x_pairs = work.tile([P, QUAD // PAIR, P, PACK, PAIR], BF16, bufs=3)
            x_words = x_blocks[(b, vb)][:].bitcast(F32).rearrange("p k (v w) -> p v k w", w=T // PAIR)
            nc.scalar.copy(
                out=x_pairs[:].bitcast(F32).rearrange("p w v k e -> p v k (w e)"),
                in_=x_words[:, :, :, quad * QUAD // PAIR : (quad + 1) * QUAD // PAIR],
            )
            unit_x_pairs[u] = x_pairs

        def load_cheb(u):
            b, quad, vb = UNITS[u]
            cheb_rows = work.tile([P, QUAD, C_OUT], BF16, bufs=6)
            nc.sync.dma_start(
                out=cheb_rows[:],
                in_=cheb01[b, quad * QUAD : (quad + 1) * QUAD, vb * P : (vb + 1) * P, :].rearrange("t v o -> v t o"),
            )
            unit_cheb_rows[u] = cheb_rows

        def turn_cheb(u):
            cheb_bank = banks.tile([P, QUAD, P], BF16, tag="turn")
            for i in range(QUAD):
                nc.tensor.transpose(cheb_bank[:, i, :], unit_cheb_rows[u][:, i, :], ident_bf[:])
            unit_cheb_bank[u] = cheb_bank

        def keep_cheb(u):
            cheb_t = work.tile([P, QUAD, P], BF16, bufs=6)
            nc.scalar.copy(out=cheb_t[:], in_=unit_cheb_bank[u][:])
            unit_cheb_t[u] = cheb_t

        def first_matmul(u, i):
            vb = UNITS[u][2]
            v_cols = slice(vb * P, (vb + 1) * P)
            g = u // N_BLOCKS
            product = banks.tile([P, PACK, P], F32, tag="first", bufs=QUAD)
            for k in range(PACK):
                c_cols = slice(k * P, (k + 1) * P)
                nc.tensor.matmul_mx(
                    out=product[:, k, :],
                    lhsT=quad_codes[g][:, i, c_cols].bitcast(FP8X4),
                    lhsT_scale=quad_scales[g][:, i, c_cols],
                    rhs=s_codes[:, v_cols].bitcast(FP8X4),
                    rhs_scale=s_scales[:, v_cols],
                    start=True,
                    stop=True,
                )
            unit_products[(u, i)] = product

        def parts_of(u):
            return [slice(0, HALF), slice(HALF, P)] if u == LAST else [slice(0, P)]

        def part_columns(u, part):
            return slice(part.start * QUAD, part.stop * QUAD)

        def subtract_x(u, i, part):
            if u not in unit_grouped:
                tx2_grouped = work.tile([P, QUAD * P, PACK], BF16, align_bytes=64)
                unit_grouped[u] = tx2_grouped
            nc.vector.scalar_tensor_tensor(
                out=unit_grouped[u][:, part_columns(u, part), :].rearrange("p (i v) k -> p i v k", i=QUAD)[:, i, :, :],
                in0=unit_products[(u, i)][:, :, part].rearrange("p k v -> p v k"),
                scalar=2.0,
                in1=unit_x_pairs[u][:, i // PAIR, part, :, i % PAIR],
                op0=ALU.mult,
                op1=ALU.subtract,
            )

        def quantise_unit(u, part):
            if u not in unit_codes:
                tx2_codes = work.tile([P, QUAD * P], U32, align_bytes=64)
                tx2_scales = work.tile([P, QUAD * P], U8, align_bytes=64)
                mixed = banks.tile([P, QUAD * P], F32, tag="small")
                unit_codes[u], unit_scales[u], unit_mixed[u] = tx2_codes, tx2_scales, mixed
            cols = part_columns(u, part)
            quantise(nc, unit_codes[u][:, cols], unit_scales[u][:, cols], unit_grouped[u][:, cols, :].rearrange("p n k -> p (n k)"))

        def second_matmul(u, part):
            cols = part_columns(u, part)
            nc.tensor.matmul_mx(
                out=unit_mixed[u][:, cols],
                lhsT=w_codes[:].bitcast(FP8X4),
                lhsT_scale=w_scales[:],
                rhs=unit_codes[u][:, cols].bitcast(FP8X4),
                rhs_scale=unit_scales[u][:, cols],
                start=True,
                stop=True,
            )

        def bias_unit(u):
            biased = work.tile([P, P, QUAD], F32, bufs=3)
            nc.scalar.activation(
                out=biased[:],
                in_=unit_mixed[u][:].rearrange("o (i v) -> o v i", i=QUAD),
                func=ACT.Identity,
                bias=bias_col[:, 0:1],
            )
            unit_biased[u] = biased

        def out_steps_of(u):
            b, quad, vb = UNITS[u]
            if quad == 0:
                out_block = out_pool.tile([P, P, T], F32)
                out_blocks[(b, vb)] = out_block
            return out_blocks[(b, vb)][:, :, quad * QUAD : (quad + 1) * QUAD]

        def wait_on_gpsimd(u):
            gate = work.tile([P, 1], U32)
            nc.gpsimd.tensor_copy(out=gate[:], in_=unit_codes[u][:, 0:1])

        def add_cheb(u):
            nc.gpsimd.tensor_tensor(
                out=out_steps_of(u),
                in0=unit_biased[u][:],
                in1=unit_cheb_t[u][:].rearrange("o i v -> o v i"),
                op=ALU.add,
            )
            store_part(u, slice(0, P))

        def finish_on_vector(u, part):
            nc.vector.scalar_tensor_tensor(
                out=out_steps_of(u)[:, part, :],
                in0=unit_mixed[u][:, part_columns(u, part)].rearrange("o (i v) -> o v i", i=QUAD),
                scalar=bias_col[:, 0:1],
                in1=unit_cheb_t[u][:, :, part].rearrange("o i v -> o v i"),
                op0=ALU.add,
                op1=ALU.add,
            )
            store_part(u, part)

        def store_part(u, part):
            b, quad, vb = UNITS[u]
            if quad == N_QUADS - 1:
                nc.sync.dma_start(
                    out=out[b, :, vb * P + part.start : vb * P + part.stop, :], in_=out_blocks[(b, vb)][:, part, :]
                )

        adj_rows = setup.tile([P, PACK, N], BF16)
        nc.sync.dma_start(out=adj_rows[:], in_=adj_param.rearrange("(p j) w -> p j w", j=PACK))
        for s in range(QUAD):
            load_step(s)
        load_x(0, 0)
        w_rows = setup.tile([P, PACK, C_OUT], BF16)
        nc.sync.dma_start(out=w_rows[:], in_=w_cheb2.rearrange("(k p) o -> p k o", p=P))
        bias_rows = setup.tile([P, P], BF16)
        nc.vector.memset(bias_rows[:], 0.0)
        nc.sync.dma_start(out=bias_rows[0:1, :], in_=cheb_bias.rearrange("(r o) -> r o", r=1))
        load_cheb(0)
        load_step(4)
        load_cheb(1)
        load_x(0, 1)
        load_cheb(2)
        load_cheb(3)
        load_x(0, 2)
        load_step(5)
        load_x(0, 3)
        load_step(6)
        load_step(7)
        load_cheb(4)
        load_step(8)

        make_identity(nc, ident_f32[:])
        make_identity(nc, ident_bf[:])

        regroup_step(0, 0, C_IN)
        quantise_step(0)

        sig = setup.tile([P, PACK, PACK, P], F32)
        sig_t = []
        for cls in range(PACK):
            nc.scalar.activation(
                out=sig[:, cls, :, :],
                in_=adj_rows[:].rearrange("q jj (m cls) -> q cls jj m", cls=PACK)[:, cls, :, :],
                func=ACT.Sigmoid,
            )
            nc.gpsimd.affine_select(
                out=sig[:, cls, cls, :],
                in_=sig[:, cls, cls, :],
                compare_op=ALU.not_equal,
                fill=0.0,
                base=0,
                pattern=[[-1, P]],
                channel_multiplier=1,
            )
            sig_t_rows = banks.tile([P, PACK, P], F32, tag="first", bufs=QUAD)
            for jj in range(PACK):
                nc.tensor.transpose(sig_t_rows[:, jj, :], sig[:, cls, jj, :], ident_f32[:])
            sig_t.append(sig_t_rows)

        root = setup.tile([P, PACK], F32)
        nc.scalar.activation(out=root[:, 0:1], in_=sig[:, PACK - 1, 0, 0:1], func=ACT.Sqrt)
        regroup_step(1, 0, C_IN)
        regroup_step(2, C_IN, 0)

        graph = setup.tile([P, PACK, N], F32)
        row_sum = setup.tile([P, PACK], F32)
        for j in range(PACK):
            nc.vector.scalar_tensor_tensor(
                out=graph[:, j, :].rearrange("p (m cls) -> p m cls", cls=PACK),
                in0=sig[:, :, j, :].rearrange("p cls m -> p m cls"),
                scalar=1.0,
                in1=sig_t[j][:].rearrange("p cls m -> p m cls"),
                op0=ALU.mult,
                op1=ALU.add,
                accum_out=row_sum[:, j : j + 1],
            )
        nc.scalar.activation(out=root[:], in_=row_sum[:], func=ACT.Sqrt)
        dis = setup.tile([P, PACK], F32)
        nc.vector.reciprocal(out=dis[:], in_=root[:])
        quantise_step(1)
        repeated = setup.tile([P, PACK, P], F32)
        nc.vector.tensor_scalar_mul(out=repeated[:], in0=dis[:].unsqueeze(2).to_broadcast([P, PACK, P]), scalar1=-1.0)
        col_factor = banks.tile([P, PACK, P], F32, tag="small")
        for jj in range(PACK):
            nc.tensor.transpose(col_factor[:, jj, :], repeated[:, jj, :], ident_f32[:])
        for v_cols in (slice(0, P), slice(P, N)):
            for j in range(PACK):
                nc.scalar.activation(out=graph[:, j, v_cols], in_=graph[:, j, v_cols], func=ACT.Copy, scale=dis[:, j : j + 1])
        pair_x(0)
        col_later = setup.tile([P, PACK, P - P // PACK], F32)
        s_grouped = setup.tile([P, N, PACK], BF16, align_bytes=64)

        def quantise_s(vb):
            v_cols = slice(vb * P, (vb + 1) * P)
            q_cols = slice((vb - 1) * P // PACK, vb * P // PACK)
            factor = col_factor[:, :, 0 : P // PACK] if vb == 0 else col_later[:, :, q_cols]
            nc.vector.tensor_tensor(
                out=s_grouped[:, v_cols, :].rearrange("p (q jj) j -> p q jj j", jj=PACK),
                in0=graph[:, :, v_cols].rearrange("p j (q jj) -> p q jj j", jj=PACK),
                in1=factor.rearrange("p jj q -> p q jj").unsqueeze(3).to_broadcast([P, P // PACK, PACK, PACK]),
                op=ALU.mult,
            )
            quantise(nc, s_codes[:, v_cols], s_scales[:, v_cols], s_grouped[:, v_cols, :].rearrange("p v j -> p (v j)"))

        def quantise_w():
            w_grouped = setup.tile([P, C_OUT, PACK], BF16, align_bytes=64)
            nc.vector.tensor_copy(out=w_grouped[:], in_=w_rows[:].rearrange("p k o -> p o k"))
            quantise(nc, w_codes[:], w_scales[:], w_grouped[:].rearrange("p o k -> p (o k)"))

        regroup_step(3, 0, C_IN)
        quantise_s(0)
        first_matmul(0, 0)
        first_matmul(0, 1)
        quantise_step(2)
        first_matmul(0, 2)
        quantise_step(3)
        first_matmul(0, 3)
        nc.scalar.copy(out=col_later[:], in_=col_factor[:, :, P // PACK :])
        regroup_step(4, C_IN, 0)
        turn_cheb(0)
        keep_cheb(0)
        bias_t = banks.tile([P, P], BF16, tag="turn")
        nc.tensor.transpose(bias_t[:], bias_rows[:], ident_bf[:])
        nc.scalar.copy(out=bias_col[:], in_=bias_t[:, 0:1])
        turn_cheb(1)

        regroup_round = {s: s - 5 for s in range(10, N_STEPS)}
        regroup_round.update({5: 2, 6: 3, 7: 3, 8: 3, 9: 4})
        quantise_round = {s: s - 4 for s in range(8, N_STEPS)}
        quantise_round.update({4: 1, 5: 3, 6: 3})

        def run_round(u):
            if u + STEP_LOAD_AHEAD < N_STEPS:
                load_step(u + STEP_LOAD_AHEAD)
            if u + UNIT_LOAD_AHEAD < N_UNITS:
                b, quad, vb = UNITS[u + UNIT_LOAD_AHEAD]
                if quad == 0:
                    load_x(b, vb)
                load_cheb(u + UNIT_LOAD_AHEAD)
            start = u < N_BLOCKS
            if not start and u < LAST:
                pair_x(u + 1)
            if 2 <= u < LAST:
                wait_on_gpsimd(u - 1)
            if 2 <= u < LAST and u % 2 == 0:
                add_cheb(u - 2)
            for part in parts_of(u):
                for i in range(QUAD):
                    subtract_x(u, i, part)
                    if u == LAST and part.start == 0 and i == 1:
                        after_gpsimd = work.tile([P, 2], F32)
                        nc.vector.tensor_copy(out=after_gpsimd[:], in_=out_blocks[(B - 1, N_BLOCKS - 2)][:, 0, 0 : 2 * QUAD : QUAD])
                        finish_on_vector(u - 1, slice(0, P))
                    if u == N_BLOCKS and i == 1:
                        quantise_step(7)
                        first_matmul(u, QUAD - 1)
                    if N_BLOCKS < u + 1 < N_UNITS and i < QUAD - 1:
                        first_matmul(u + 1, i)
                if u == LAST and part.start == 0:
                    quantise_unit(u, part)
                    second_matmul(u, part)
            for s in regroup_round:
                if regroup_round[s] == u:
                    regroup_step(s, *((192, 0) if s % 2 == 0 else (C_IN, 0) if s >= 2 * QUAD else (256, 256)))
            if start:
                pair_x(u + 1)
            if u < LAST:
                keep_cheb(u + 1)
            if 1 <= u < LAST and u % 2 == 1:
                bias_unit(u - 1)
            if 1 <= u < LAST and u % 2 == 0:
                finish_on_vector(u - 1, slice(0, P))
            if u + 1 < N_BLOCKS:
                quantise_s(u + 1)
            if u == 0:
                quantise_w()
            for s in quantise_round:
                if quantise_round[s] == u:
                    quantise_step(s)
            if u < LAST:
                for i in range(0 if u + 1 <= N_BLOCKS else QUAD - 1, QUAD):
                    if (u + 1, i) != (N_BLOCKS, QUAD - 1):
                        first_matmul(u + 1, i)
            if u + 2 < N_UNITS:
                turn_cheb(u + 2)
            if u == LAST:
                finish_on_vector(u, slice(0, HALF))
            part = parts_of(u)[-1]
            quantise_unit(u, part)
            second_matmul(u, part)
            if u == LAST:
                finish_on_vector(u, part)

        for u in range(N_UNITS):
            run_round(u)
